import numpy as np
import ml_dtypes


def mxq(x, axis, fmt="e4m3"):
    dtype, down = {"e4m3": (ml_dtypes.float8_e4m3fn, 7), "e5m2": (ml_dtypes.float8_e5m2, 14)}[fmt]
    v = np.moveaxis(np.asarray(x, np.float32).astype(ml_dtypes.bfloat16).astype(np.float64), axis, -1)
    blocks = v.reshape(v.shape[:-1] + (-1, 32))
    amax = np.abs(blocks).max(-1, keepdims=True)
    byte = np.maximum(np.where(amax > 0, np.frexp(amax)[1] - 1 + 127, 0) - down, 1)
    scale = np.exp2(byte - 127.0)
    codes = (blocks / scale).astype(np.float32).astype(dtype).astype(np.float64)
    return np.moveaxis((codes * scale).reshape(v.shape), -1, axis)


WIDE = False


def mx_kscale(k):
    if not WIDE:
        return np.ones(k)
    levels = np.array([10, -10, 5, -5, 0])
    a = np.random.permutation(np.resize(levels, k // 512 * 4)).reshape(k // 512, 4)
    idx = np.arange(k)
    return np.exp2(a[idx // 512, idx % 128 // 32])


BF16 = ml_dtypes.bfloat16


def bf(x):
    return np.asarray(x, np.float32).astype(BF16)


def f64(x):
    return np.asarray(x).astype(np.float64)


N, E, C, D1, D2 = 1024, 2048, 512, 2, 2
T2 = D2 + 1


def shift_down(y, k):
    return np.pad(y, ((k, 0), (0, 0)))[:y.shape[0]] if k > 0 else y


def log_softmax(z):
    d = z - z.max(-1, keepdims=True)
    return d - np.log(np.exp(d).sum(-1, keepdims=True))


def setup_inputs():
    s = mx_kscale(C)
    return {"H": bf(np.tanh(np.random.standard_normal((N, C))) * s),
            "W2": bf(np.random.standard_normal((T2, C, C)) * 2.0 / np.sqrt(C) / s[None, :, None]),
            "b2": bf(np.random.standard_normal((1, C)) * 0.2)}


def reference(H, W2, b2):
    G = mxq(f64(H), 1, "e4m3") @ mxq(f64(W2), 1, "e4m3")
    Z = sum(shift_down(G[j], D2 - j) for j in range(T2)) + T2 * f64(b2)[0]
    return log_softmax(Z)

@@ -1,0 +1,196 @@
+from contextlib import ExitStack
+
+import concourse.mybir as mybir
+from concourse.masks import make_identity
+
+F32 = mybir.dt.float32
+BF16 = mybir.dt.bfloat16
+U32 = mybir.dt.uint32
+U8 = mybir.dt.uint8
+FP8X4 = mybir.dt.float8_e4m3fn_x4
+ALU = mybir.AluOpType
+ACT = mybir.ActivationFunctionType
+AX = mybir.AxisListType
+
+P = 128
+ROWS = 1024
+K = 512
+C = 512
+TAPS = 3
+R = 8
+FLOPS = 2 * ROWS * K * C * TAPS
+
+V_COLS = 320
+GROUPS = ((0, 4), (4, 8))
+
+
+def tile_predictor_pb_kernel(tc, H, W2, b2, out):
+    nc = tc.nc
+    with ExitStack() as ctx:
+        keep = ctx.enter_context(tc.tile_pool(name="keep", bufs=1))
+        psum = ctx.enter_context(tc.psum_pool(name="psum", bufs=8))
+
+        ident = keep.tile([P, P], F32, name="ident")
+        make_identity(nc, ident[:])
+
+        h_sb = keep.tile([P, R, K], BF16, name="h_sb")
+        w_raw = keep.tile([P, TAPS, 4, C], BF16, name="w_raw")
+        b_row = keep.tile([P, C], BF16, name="b_row")
+        threes = keep.tile([P, P], BF16, name="threes")
+        bias = keep.tile([P, C], F32, name="bias")
+        h_grp = keep.tile([P, R, P, 4], BF16, name="h_grp", align_bytes=64)
+        h_grp_s = keep.tile([P, 2, P, 4], BF16, name="h_grp_s", align_bytes=64)
+        w_grp = keep.tile([P, TAPS, C, 4], BF16, name="w_grp", align_bytes=64)
+        h_codes = keep.tile([P, R + 2, P], U32, name="h_codes", align_bytes=64)
+        h_scales = keep.tile([P, R + 2, P], U8, name="h_scales", align_bytes=64)
+        w_codes = keep.tile([P, TAPS, C], U32, name="w_codes", align_bytes=64)
+        w_scales = keep.tile([P, TAPS, C], U8, name="w_scales", align_bytes=64)
+        z = keep.tile([P, R, C], F32, name="z")
+        junk = keep.tile([P, C], BF16, name="junk")
+        nm = keep.tile([P, R], F32, name="nm")
+        s = keep.tile([P, R], F32, name="s")
+        l = keep.tile([P, R], F32, name="l")
+        d = keep.tile([P, R], F32, name="d")
+
+        nc.vector.memset(b_row[:], 0.0)
+        nc.vector.memset(threes[:], 3.0)
+        nc.vector.memset(h_grp_s[:], 0.0)
+
+        h_view = H.rearrange("(m r) k -> m r k", r=R)
+        out_view = out.rearrange("(m r) c -> m r c", r=R)
+
+        def load_h(a):
+            nc.sync.dma_start(out=h_sb[:, 2 * a : 2 * a + 2, :], in_=h_view[:, 2 * a : 2 * a + 2, :])
+
+        def load_w(j):
+            nc.sync.dma_start(
+                out=w_raw[:, j].rearrange("p (u e) c -> p u e c", u=2),
+                in_=W2[j].rearrange("(u q e) c -> q u e c", u=2, e=2),
+            )
+
+        nc.scalar.dma_start(out=b_row[0:1, :], in_=b2)
+        load_h(3)
+        load_h(0)
+        load_w(0)
+        load_w(1)
+        load_w(2)
+        load_h(1)
+        load_h(2)
+
+        b_ps = psum.tile([P, C], F32, name="b_ps", tag="bank")
+        nc.tensor.matmul(b_ps[:], lhsT=threes[:], rhs=b_row[:], start=True, stop=True)
+        nc.scalar.copy(out=bias[:], in_=b_ps[:])
+
+        h_words = h_sb[:].bitcast(F32)
+        h_grp_w = h_grp[:].bitcast(F32)
+        h_grp_s_w = h_grp_s[:].bitcast(F32)
+
+        def quant_h(src, t0):
+            nc.vector.quantize_mx(
+                out=h_codes[:, t0 : t0 + 2, :].rearrange("p r m -> p (r m)").bitcast(FP8X4),
+                scales=h_scales[:, t0 : t0 + 2, :].rearrange("p r m -> p (r m)"),
+                in_=src.rearrange("p r m t -> p (r m t)"),
+            )
+
+        def prep_h(a):
+            xt = psum.tile([P, 2, 2, P], F32, name="xt", tag="bank")
+            for r2 in range(2):
+                for u in range(2):
+                    nc.tensor.transpose(
+                        xt[:, r2, u, :], h_words[:, 2 * a + r2, P * u : P * u + P], ident[:]
+                    )
+            nc.scalar.copy(
+                out=h_grp_w[:, 2 * a : 2 * a + 2, :, :], in_=xt[:].rearrange("p r u m -> p r m u")
+            )
+            if a == 3:
+                nc.vector.tensor_copy(
+                    out=h_grp_s_w[:, :, 1:P, :],
+                    in_=xt[:, :, :, 0 : P - 1].rearrange("p r u m -> p r m u"),
+                )
+                quant_h(h_grp_s[:], R)
+            quant_h(h_grp[:, 2 * a : 2 * a + 2], 2 * a)
+
+        def prep_w(j):
+            for copy, c0, c1 in (
+                (nc.vector.tensor_copy, 0, V_COLS),
+                (nc.scalar.copy, V_COLS, C),
+            ):
+                copy(
+                    out=w_grp[:, j, c0:c1, :].rearrange("p (c i) t -> p c t i", i=4),
+                    in_=w_raw[:, j, :, c0:c1].rearrange("p t (c i) -> p c t i", i=4),
+                )
+            nc.vector.quantize_mx(
+                out=w_codes[:, j, :].bitcast(FP8X4),
+                scales=w_scales[:, j, :],
+                in_=w_grp[:, j].rearrange("p c t -> p (c t)"),
+            )
+
+        def tile_rows(r):
+            z_ps = psum.tile([P, C], F32, name="z_ps", tag="bank")
+            for j in range(TAPS):
+                src = r - (TAPS - 1 - j)
+                idx = src if src >= 0 else R + 2 + src
+                nc.tensor.matmul_mx(
+                    out=z_ps[:],
+                    lhsT=h_codes[:, idx, :].bitcast(FP8X4),
+                    lhsT_scale=h_scales[:, idx, :],
+                    rhs=w_codes[:, j, :].bitcast(FP8X4),
+                    rhs_scale=w_scales[:, j, :],
+                    start=(j == 0),
+                    stop=(j == TAPS - 1),
+                )
+            nc.vector.tensor_tensor(out=z[:, r, :], in0=z_ps[:], in1=bias[:], op=ALU.add)
+            nc.vector.tensor_reduce(
+                out=nm[:, r : r + 1], in_=z[:, r, :], axis=AX.X, op=ALU.max, negate=True
+            )
+            nc.scalar.activation(
+                out=junk[:],
+                in_=z[:, r, :],
+                func=ACT.Exp,
+                bias=nm[:, r : r + 1],
+                scale=1.0,
+                accum_out=s[:, r : r + 1],
+            )
+
+        def finish(g, g0, g1):
+            nc.scalar.activation(out=l[:, g0:g1], in_=s[:, g0:g1], func=ACT.Ln)
+            if g == 0:
+                nc.gpsimd.tensor_tensor(
+                    out=d[:, g0:g1], in0=nm[:, g0:g1], in1=l[:, g0:g1], op=ALU.subtract
+                )
+            for r in range(g0, g1):
+                if g == 0:
+                    nc.gpsimd.tensor_scalar(
+                        out=z[:, r, :],
+                        in0=z[:, r, :],
+                        scalar1=d[:, r : r + 1],
+                        scalar2=1.0,
+                        op0=ALU.add,
+                        op1=ALU.mult,
+                    )
+                else:
+                    nc.vector.tensor_scalar(
+                        out=z[:, r, :],
+                        in0=z[:, r, :],
+                        scalar1=nm[:, r : r + 1],
+                        scalar2=l[:, r : r + 1],
+                        op0=ALU.add,
+                        op1=ALU.subtract,
+                    )
+                nc.sync.dma_start(out=out_view[:, r, :], in_=z[:, r, :])
+
+        prep_h(3)
+        prep_h(0)
+        prep_w(0)
+        prep_w(1)
+        prep_w(2)
+        prep_h(1)
+        tile_rows(0)
+        tile_rows(1)
+        prep_h(2)
+        tile_rows(2)
+        tile_rows(3)
+        finish(0, 0, 4)
+        for r in range(4, 8):
+            tile_rows(r)
+        finish(1, 4, 8)

@@ -20,8 +20,8 @@ TAPS = 3
 R = 8
 FLOPS = 2 * ROWS * K * C * TAPS
 
-V_COLS = 320
-GROUPS = ((0, 4), (4, 8))
+V_COLS = 256
+SPLIT = 3
 
 
 def tile_predictor_pb_kernel(tc, H, W2, b2, out):
@@ -29,6 +29,7 @@ def tile_predictor_pb_kernel(tc, H, W2, b2, out):
     with ExitStack() as ctx:
         keep = ctx.enter_context(tc.tile_pool(name="keep", bufs=1))
         psum = ctx.enter_context(tc.psum_pool(name="psum", bufs=8))
+        ctx.enter_context(tc.manual_schedule())
 
         ident = keep.tile([P, P], F32, name="ident")
         make_identity(nc, ident[:])
@@ -68,7 +69,7 @@ def tile_predictor_pb_kernel(tc, H, W2, b2, out):
                 in_=W2[j].rearrange("(u q e) c -> q u e c", u=2, e=2),
             )
 
-        nc.scalar.dma_start(out=b_row[0:1, :], in_=b2)
+        nc.sync.dma_start(out=b_row[0:1, :], in_=b2)
         load_h(3)
         load_h(0)
         load_w(0)
@@ -92,7 +93,7 @@ def tile_predictor_pb_kernel(tc, H, W2, b2, out):
                 in_=src.rearrange("p r m t -> p (r m t)"),
             )
 
-        def prep_h(a):
+        def transposes(a):
             xt = psum.tile([P, 2, 2, P], F32, name="xt", tag="bank")
             for r2 in range(2):
                 for u in range(2):
@@ -102,15 +103,9 @@ def tile_predictor_pb_kernel(tc, H, W2, b2, out):
             nc.scalar.copy(
                 out=h_grp_w[:, 2 * a : 2 * a + 2, :, :], in_=xt[:].rearrange("p r u m -> p r m u")
             )
-            if a == 3:
-                nc.vector.tensor_copy(
-                    out=h_grp_s_w[:, :, 1:P, :],
-                    in_=xt[:, :, :, 0 : P - 1].rearrange("p r u m -> p r m u"),
-                )
-                quant_h(h_grp_s[:], R)
-            quant_h(h_grp[:, 2 * a : 2 * a + 2], 2 * a)
+            return xt
 
-        def prep_w(j):
+        def regroup_w(j):
             for copy, c0, c1 in (
                 (nc.vector.tensor_copy, 0, V_COLS),
                 (nc.scalar.copy, V_COLS, C),
@@ -119,13 +114,15 @@ def tile_predictor_pb_kernel(tc, H, W2, b2, out):
                     out=w_grp[:, j, c0:c1, :].rearrange("p (c i) t -> p c t i", i=4),
                     in_=w_raw[:, j, :, c0:c1].rearrange("p t (c i) -> p c t i", i=4),
                 )
+
+        def quant_w(j):
             nc.vector.quantize_mx(
                 out=w_codes[:, j, :].bitcast(FP8X4),
                 scales=w_scales[:, j, :],
                 in_=w_grp[:, j].rearrange("p c t -> p (c t)"),
             )
 
-        def tile_rows(r):
+        def passes(r):
             z_ps = psum.tile([P, C], F32, name="z_ps", tag="bank")
             for j in range(TAPS):
                 src = r - (TAPS - 1 - j)
@@ -139,6 +136,9 @@ def tile_predictor_pb_kernel(tc, H, W2, b2, out):
                     start=(j == 0),
                     stop=(j == TAPS - 1),
                 )
+            return z_ps
+
+        def softmax_sums(r, z_ps):
             nc.vector.tensor_tensor(out=z[:, r, :], in0=z_ps[:], in1=bias[:], op=ALU.add)
             nc.vector.tensor_reduce(
                 out=nm[:, r : r + 1], in_=z[:, r, :], axis=AX.X, op=ALU.max, negate=True
@@ -152,14 +152,14 @@ def tile_predictor_pb_kernel(tc, H, W2, b2, out):
                 accum_out=s[:, r : r + 1],
             )
 
-        def finish(g, g0, g1):
+        def finish(early, g0, g1):
             nc.scalar.activation(out=l[:, g0:g1], in_=s[:, g0:g1], func=ACT.Ln)
-            if g == 0:
+            if early:
                 nc.gpsimd.tensor_tensor(
                     out=d[:, g0:g1], in0=nm[:, g0:g1], in1=l[:, g0:g1], op=ALU.subtract
                 )
             for r in range(g0, g1):
-                if g == 0:
+                if early:
                     nc.gpsimd.tensor_scalar(
                         out=z[:, r, :],
                         in0=z[:, r, :],
@@ -179,18 +179,31 @@ def tile_predictor_pb_kernel(tc, H, W2, b2, out):
                     )
                 nc.sync.dma_start(out=out_view[:, r, :], in_=z[:, r, :])
 
-        prep_h(3)
-        prep_h(0)
-        prep_w(0)
-        prep_w(1)
-        prep_w(2)
-        prep_h(1)
-        tile_rows(0)
-        tile_rows(1)
-        prep_h(2)
-        tile_rows(2)
-        tile_rows(3)
-        finish(0, 0, 4)
-        for r in range(4, 8):
-            tile_rows(r)
-        finish(1, 4, 8)
+        xt3 = transposes(3)
+        nc.vector.tensor_copy(
+            out=h_grp_s_w[:, :, 1:P, :],
+            in_=xt3[:, :, :, 0 : P - 1].rearrange("p r u m -> p r m u"),
+        )
+        transposes(0)
+        quant_h(h_grp_s[:], R)
+        quant_h(h_grp[:, 6:8], 6)
+        regroup_w(0)
+        quant_h(h_grp[:, 0:2], 0)
+        regroup_w(1)
+        quant_w(0)
+        regroup_w(2)
+        quant_w(1)
+        transposes(1)
+        transposes(2)
+        quant_w(2)
+        quant_h(h_grp[:, 2:4], 2)
+        banks = [passes(0), passes(1)]
+        softmax_sums(0, banks[0])
+        quant_h(h_grp[:, 4:6], 4)
+        for r in range(2, R):
+            banks.append(passes(r))
+        for r in range(1, R):
+            softmax_sums(r, banks[r])
+            if r == SPLIT - 1:
+                finish(True, 0, SPLIT)
+        finish(False, SPLIT, R)

@@ -21,7 +21,7 @@ R = 8
 FLOPS = 2 * ROWS * K * C * TAPS
 
 V_COLS = 256
-SPLIT = 3
+SPLIT = 2
 
 
 def tile_predictor_pb_kernel(tc, H, W2, b2, out):
@@ -69,18 +69,14 @@ def tile_predictor_pb_kernel(tc, H, W2, b2, out):
                 in_=W2[j].rearrange("(u q e) c -> q u e c", u=2, e=2),
             )
 
-        nc.sync.dma_start(out=b_row[0:1, :], in_=b2)
         load_h(3)
         load_h(0)
+        nc.sync.dma_start(out=b_row[0:1, :], in_=b2)
         load_w(0)
         load_w(1)
         load_w(2)
         load_h(1)
         load_h(2)
-
-        b_ps = psum.tile([P, C], F32, name="b_ps", tag="bank")
-        nc.tensor.matmul(b_ps[:], lhsT=threes[:], rhs=b_row[:], start=True, stop=True)
-        nc.scalar.copy(out=bias[:], in_=b_ps[:])
 
         h_words = h_sb[:].bitcast(F32)
         h_grp_w = h_grp[:].bitcast(F32)
@@ -138,8 +134,10 @@ def tile_predictor_pb_kernel(tc, H, W2, b2, out):
                 )
             return z_ps
 
-        def softmax_sums(r, z_ps):
+        def add_bias(r, z_ps):
             nc.vector.tensor_tensor(out=z[:, r, :], in0=z_ps[:], in1=bias[:], op=ALU.add)
+
+        def softmax_sums(r):
             nc.vector.tensor_reduce(
                 out=nm[:, r : r + 1], in_=z[:, r, :], axis=AX.X, op=ALU.max, negate=True
             )
@@ -185,6 +183,9 @@ def tile_predictor_pb_kernel(tc, H, W2, b2, out):
             in_=xt3[:, :, :, 0 : P - 1].rearrange("p r u m -> p r m u"),
         )
         transposes(0)
+        b_ps = psum.tile([P, C], F32, name="b_ps", tag="bank")
+        nc.tensor.matmul(b_ps[:], lhsT=threes[:], rhs=b_row[:], start=True, stop=True)
+        nc.scalar.copy(out=bias[:], in_=b_ps[:])
         quant_h(h_grp_s[:], R)
         quant_h(h_grp[:, 6:8], 6)
         regroup_w(0)
@@ -198,12 +199,14 @@ def tile_predictor_pb_kernel(tc, H, W2, b2, out):
         quant_w(2)
         quant_h(h_grp[:, 2:4], 2)
         banks = [passes(0), passes(1)]
-        softmax_sums(0, banks[0])
+        add_bias(0, banks[0])
         quant_h(h_grp[:, 4:6], 4)
         for r in range(2, R):
             banks.append(passes(r))
-        for r in range(1, R):
-            softmax_sums(r, banks[r])
-            if r == SPLIT - 1:
+        for r in range(1, R + 1):
+            if r < R:
+                add_bias(r, banks[r])
+            softmax_sums(r - 1)
+            if r == SPLIT:
                 finish(True, 0, SPLIT)
         finish(False, SPLIT, R)

@@ -64,10 +64,7 @@ def tile_predictor_pb_kernel(tc, H, W2, b2, out):
             nc.sync.dma_start(out=h_sb[:, 2 * a : 2 * a + 2, :], in_=h_view[:, 2 * a : 2 * a + 2, :])
 
         def load_w(j):
-            nc.sync.dma_start(
-                out=w_raw[:, j].rearrange("p (u e) c -> p u e c", u=2),
-                in_=W2[j].rearrange("(u q e) c -> q u e c", u=2, e=2),
-            )
+            nc.sync.dma_start(out=w_raw[:, j], in_=W2[j].rearrange("(p t) c -> p t c", t=4))
 
         load_h(3)
         load_h(0)
@@ -78,7 +75,7 @@ def tile_predictor_pb_kernel(tc, H, W2, b2, out):
         load_h(1)
         load_h(2)
 
-        h_words = h_sb[:].bitcast(F32)
+        h_words = h_sb[:].bitcast(F32).rearrange("m r (p u) -> m r u p", u=2)
         h_grp_w = h_grp[:].bitcast(F32)
         h_grp_s_w = h_grp_s[:].bitcast(F32)
 
@@ -94,7 +91,7 @@ def tile_predictor_pb_kernel(tc, H, W2, b2, out):
             for r2 in range(2):
                 for u in range(2):
                     nc.tensor.transpose(
-                        xt[:, r2, u, :], h_words[:, 2 * a + r2, P * u : P * u + P], ident[:]
+                        xt[:, r2, u, :], h_words[:, 2 * a + r2, u, :], ident[:]
                     )
             nc.scalar.copy(
                 out=h_grp_w[:, 2 * a : 2 * a + 2, :, :], in_=xt[:].rearrange("p r u m -> p r m u")
@@ -183,9 +180,6 @@ def tile_predictor_pb_kernel(tc, H, W2, b2, out):
             in_=xt3[:, :, :, 0 : P - 1].rearrange("p r u m -> p r m u"),
         )
         transposes(0)
-        b_ps = psum.tile([P, C], F32, name="b_ps", tag="bank")
-        nc.tensor.matmul(b_ps[:], lhsT=threes[:], rhs=b_row[:], start=True, stop=True)
-        nc.scalar.copy(out=bias[:], in_=b_ps[:])
         quant_h(h_grp_s[:], R)
         quant_h(h_grp[:, 6:8], 6)
         regroup_w(0)
@@ -196,6 +190,9 @@ def tile_predictor_pb_kernel(tc, H, W2, b2, out):
         quant_w(1)
         transposes(1)
         transposes(2)
+        b_ps = psum.tile([P, C], F32, name="b_ps", tag="bank")
+        nc.tensor.matmul(b_ps[:], lhsT=threes[:], rhs=b_row[:], start=True, stop=True)
+        nc.scalar.copy(out=bias[:], in_=b_ps[:])
         quant_w(2)
         quant_h(h_grp[:, 2:4], 2)
         banks = [passes(0), passes(1)]

@@ -1,3 +1,4 @@
+import math
 from contextlib import ExitStack
 
 import concourse.mybir as mybir
@@ -21,7 +22,14 @@ R = 8
 FLOPS = 2 * ROWS * K * C * TAPS
 
 V_COLS = 256
-SPLIT = 2
+
+EULER = 2.718281828459045
+N_THR = 128
+LN_STEP = (math.log(512.0) + 1.0e-3) / (N_THR + 0.5)
+LN_C2 = -0.5
+LN_C3 = 0.3334271013736725
+LN_C4 = -0.25007814168930054
+LEVELS = 7
 
 
 def tile_predictor_pb_kernel(tc, H, W2, b2, out):
@@ -50,12 +58,31 @@ def tile_predictor_pb_kernel(tc, H, W2, b2, out):
         junk = keep.tile([P, C], BF16, name="junk")
         nm = keep.tile([P, R], F32, name="nm")
         s = keep.tile([P, R], F32, name="s")
-        l = keep.tile([P, R], F32, name="l")
+        consts = keep.tile([P, 4], F32, name="consts")
+        thr = keep.tile([P, N_THR], F32, name="thr")
+        junk_t = keep.tile([P, N_THR], BF16, name="junk_t")
+        cnt = keep.tile([P, R], F32, name="cnt")
+        ch = keep.tile([P, R, 8], F32, name="ch")
+        w = keep.tile([P, R], F32, name="w")
         d = keep.tile([P, R], F32, name="d")
 
         nc.vector.memset(b_row[:], 0.0)
         nc.vector.memset(threes[:], 3.0)
         nc.vector.memset(h_grp_s[:], 0.0)
+        nc.vector.memset(consts[:, 0:1], -LN_STEP * N_THR / 2.0)
+        nc.vector.memset(consts[:, 1:2], -1.0)
+        nc.vector.memset(consts[:, 2:3], -LN_C3)
+        nc.vector.memset(consts[:, 3:4], -LN_C2)
+        nc.gpsimd.memset(thr[:, 0:1], EULER ** (LN_STEP / 2.0))
+        for width in (1, 2, 4, 8, 16, 32, 64):
+            nc.gpsimd.tensor_scalar(
+                out=thr[:, width : 2 * width],
+                in0=thr[:, 0:width],
+                scalar1=EULER ** (LN_STEP * width),
+                scalar2=0.0,
+                op0=ALU.mult,
+                op1=ALU.add,
+            )
 
         h_view = H.rearrange("(m r) k -> m r k", r=R)
         out_view = out.rearrange("(m r) c -> m r c", r=R)
@@ -134,10 +161,12 @@ def tile_predictor_pb_kernel(tc, H, W2, b2, out):
         def add_bias(r, z_ps):
             nc.vector.tensor_tensor(out=z[:, r, :], in0=z_ps[:], in1=bias[:], op=ALU.add)
 
-        def softmax_sums(r):
+        def row_max(r):
             nc.vector.tensor_reduce(
                 out=nm[:, r : r + 1], in_=z[:, r, :], axis=AX.X, op=ALU.max, negate=True
             )
+
+        def exp_sum(r):
             nc.scalar.activation(
                 out=junk[:],
                 in_=z[:, r, :],
@@ -147,32 +176,60 @@ def tile_predictor_pb_kernel(tc, H, W2, b2, out):
                 accum_out=s[:, r : r + 1],
             )
 
-        def finish(early, g0, g1):
-            nc.scalar.activation(out=l[:, g0:g1], in_=s[:, g0:g1], func=ACT.Ln)
-            if early:
-                nc.gpsimd.tensor_tensor(
-                    out=d[:, g0:g1], in0=nm[:, g0:g1], in1=l[:, g0:g1], op=ALU.subtract
+        def ident_act(dst, src, scale, bias):
+            nc.scalar.activation(out=dst, in_=src, func=ACT.Identity, bias=bias, scale=scale)
+
+        def chain_level(r, k, on_vector):
+            one = slice(r, r + 1)
+            nl0, e0, x, qa, qb, qc = [ch[:, r, i : i + 1] for i in range(6)]
+            if k == 0:
+                nc.scalar.activation(
+                    out=junk_t[:],
+                    in_=thr[:],
+                    func=ACT.Sign,
+                    bias=s[:, one],
+                    scale=-1.0,
+                    accum_out=cnt[:, one],
                 )
-            for r in range(g0, g1):
-                if early:
+            elif k == 1:
+                nc.scalar.activation(
+                    out=e0, in_=cnt[:, one], func=ACT.Exp, bias=consts[:, 0:1], scale=-LN_STEP / 2.0
+                )
+                ident_act(nl0, cnt[:, one], -LN_STEP / 2.0, consts[:, 0:1])
+                nc.gpsimd.tensor_tensor(out=w[:, one], in0=nm[:, one], in1=nl0, op=ALU.add)
+            elif k == 2:
+                ident_act(x, e0, s[:, one], consts[:, 1:2])
+            elif k == 3:
+                ident_act(qa, x, -LN_C4, consts[:, 2:3])
+            elif k == 4:
+                ident_act(qb, qa, x, consts[:, 3:4])
+            elif k == 5:
+                ident_act(qc, qb, x, consts[:, 1:2])
+            else:
+                ident_act(d[:, one], qc, x, w[:, one])
+                if on_vector:
+                    nc.vector.tensor_scalar(
+                        out=z[:, r, :], in0=z[:, r, :], scalar1=d[:, one], scalar2=None, op0=ALU.add
+                    )
+                else:
                     nc.gpsimd.tensor_scalar(
                         out=z[:, r, :],
                         in0=z[:, r, :],
-                        scalar1=d[:, r : r + 1],
+                        scalar1=d[:, one],
                         scalar2=1.0,
                         op0=ALU.add,
                         op1=ALU.mult,
                     )
-                else:
-                    nc.vector.tensor_scalar(
-                        out=z[:, r, :],
-                        in0=z[:, r, :],
-                        scalar1=nm[:, r : r + 1],
-                        scalar2=l[:, r : r + 1],
-                        op0=ALU.add,
-                        op1=ALU.subtract,
-                    )
                 nc.sync.dma_start(out=out_view[:, r, :], in_=z[:, r, :])
+
+        next_level = [0] * R
+        started = []
+
+        def run_round(on_vector):
+            for r in started:
+                if next_level[r] < LEVELS:
+                    chain_level(r, next_level[r], on_vector)
+                    next_level[r] = next_level[r] + 1
 
         xt3 = transposes(3)
         nc.vector.tensor_copy(
@@ -200,10 +257,13 @@ def tile_predictor_pb_kernel(tc, H, W2, b2, out):
         quant_h(h_grp[:, 4:6], 4)
         for r in range(2, R):
             banks.append(passes(r))
-        for r in range(1, R + 1):
-            if r < R:
-                add_bias(r, banks[r])
-            softmax_sums(r - 1)
-            if r == SPLIT:
-                finish(True, 0, SPLIT)
-        finish(False, SPLIT, R)
+        for r in range(R):
+            if r + 1 < R:
+                add_bias(r + 1, banks[r + 1])
+            row_max(r)
+            run_round(False)
+            exp_sum(r)
+            run_round(False)
+            started.append(r)
+        for k in range(LEVELS):
+            run_round(True)

@@ -1,4 +1,3 @@
-import math
 from contextlib import ExitStack
 
 import concourse.mybir as mybir
@@ -25,7 +24,7 @@ V_COLS = 256
 
 EULER = 2.718281828459045
 N_THR = 128
-LN_STEP = (math.log(512.0) + 1.0e-3) / (N_THR + 0.5)
+LN_STEP = 1591.0 / 32768.0
 LN_C2 = -0.5
 LN_C3 = 0.3334271013736725
 LN_C4 = -0.25007814168930054
@@ -64,6 +63,7 @@ def tile_predictor_pb_kernel(tc, H, W2, b2, out):
         cnt = keep.tile([P, R], F32, name="cnt")
         ch = keep.tile([P, R, 8], F32, name="ch")
         w = keep.tile([P, R], F32, name="w")
+        nl = keep.tile([P, R], F32, name="nl")
         d = keep.tile([P, R], F32, name="d")
 
         nc.vector.memset(b_row[:], 0.0)
@@ -91,7 +91,10 @@ def tile_predictor_pb_kernel(tc, H, W2, b2, out):
             nc.sync.dma_start(out=h_sb[:, 2 * a : 2 * a + 2, :], in_=h_view[:, 2 * a : 2 * a + 2, :])
 
         def load_w(j):
-            nc.sync.dma_start(out=w_raw[:, j], in_=W2[j].rearrange("(p t) c -> p t c", t=4))
+            nc.sync.dma_start(
+                out=w_raw[:, j].rearrange("p (u e) c -> p u e c", u=2),
+                in_=W2[j].rearrange("(u q e) c -> q u e c", u=2, e=2),
+            )
 
         load_h(3)
         load_h(0)
@@ -102,7 +105,7 @@ def tile_predictor_pb_kernel(tc, H, W2, b2, out):
         load_h(1)
         load_h(2)
 
-        h_words = h_sb[:].bitcast(F32).rearrange("m r (p u) -> m r u p", u=2)
+        h_words = h_sb[:].bitcast(F32).rearrange("m r (u p) -> m r u p", u=2)
         h_grp_w = h_grp[:].bitcast(F32)
         h_grp_s_w = h_grp_s[:].bitcast(F32)
 
@@ -120,10 +123,12 @@ def tile_predictor_pb_kernel(tc, H, W2, b2, out):
                     nc.tensor.transpose(
                         xt[:, r2, u, :], h_words[:, 2 * a + r2, u, :], ident[:]
                     )
+            return xt
+
+        def copy_out(a, xt):
             nc.scalar.copy(
                 out=h_grp_w[:, 2 * a : 2 * a + 2, :, :], in_=xt[:].rearrange("p r u m -> p r m u")
             )
-            return xt
 
         def regroup_w(j):
             for copy, c0, c1 in (
@@ -142,20 +147,21 @@ def tile_predictor_pb_kernel(tc, H, W2, b2, out):
                 in_=w_grp[:, j].rearrange("p c t -> p (c t)"),
             )
 
-        def passes(r):
+        def mx_pass(r, j, z_ps):
+            src = r - (TAPS - 1 - j)
+            idx = src if src >= 0 else R + 2 + src
+            nc.tensor.matmul_mx(
+                out=z_ps[:],
+                lhsT=h_codes[:, idx, :].bitcast(FP8X4),
+                lhsT_scale=h_scales[:, idx, :],
+                rhs=w_codes[:, j, :].bitcast(FP8X4),
+                rhs_scale=w_scales[:, j, :],
+                start=(j == 0),
+                stop=(j == TAPS - 1),
+            )
+
+        def new_bank():
             z_ps = psum.tile([P, C], F32, name="z_ps", tag="bank")
-            for j in range(TAPS):
-                src = r - (TAPS - 1 - j)
-                idx = src if src >= 0 else R + 2 + src
-                nc.tensor.matmul_mx(
-                    out=z_ps[:],
-                    lhsT=h_codes[:, idx, :].bitcast(FP8X4),
-                    lhsT_scale=h_scales[:, idx, :],
-                    rhs=w_codes[:, j, :].bitcast(FP8X4),
-                    rhs_scale=w_scales[:, j, :],
-                    start=(j == 0),
-                    stop=(j == TAPS - 1),
-                )
             return z_ps
 
         def add_bias(r, z_ps):
@@ -181,7 +187,8 @@ def tile_predictor_pb_kernel(tc, H, W2, b2, out):
 
         def chain_level(r, k, on_vector):
             one = slice(r, r + 1)
-            nl0, e0, x, qa, qb, qc = [ch[:, r, i : i + 1] for i in range(6)]
+            nl0 = nl[:, one]
+            e0, x, qa, qb, qc = [ch[:, r, i : i + 1] for i in range(5)]
             if k == 0:
                 nc.scalar.activation(
                     out=junk_t[:],
@@ -195,7 +202,14 @@ def tile_predictor_pb_kernel(tc, H, W2, b2, out):
                 nc.scalar.activation(
                     out=e0, in_=cnt[:, one], func=ACT.Exp, bias=consts[:, 0:1], scale=-LN_STEP / 2.0
                 )
-                ident_act(nl0, cnt[:, one], -LN_STEP / 2.0, consts[:, 0:1])
+                nc.gpsimd.tensor_scalar(
+                    out=nl0,
+                    in0=cnt[:, one],
+                    scalar1=float(N_THR),
+                    scalar2=-LN_STEP / 2.0,
+                    op0=ALU.add,
+                    op1=ALU.mult,
+                )
                 nc.gpsimd.tensor_tensor(out=w[:, one], in0=nm[:, one], in1=nl0, op=ALU.add)
             elif k == 2:
                 ident_act(x, e0, s[:, one], consts[:, 1:2])
@@ -232,35 +246,49 @@ def tile_predictor_pb_kernel(tc, H, W2, b2, out):
                     next_level[r] = next_level[r] + 1
 
         xt3 = transposes(3)
+        copy_out(3, xt3)
         nc.vector.tensor_copy(
             out=h_grp_s_w[:, :, 1:P, :],
             in_=xt3[:, :, :, 0 : P - 1].rearrange("p r u m -> p r m u"),
         )
-        transposes(0)
+        copy_out(0, transposes(0))
+        b_ps = psum.tile([P, C], F32, name="b_ps", tag="bank")
+        nc.tensor.matmul(b_ps[:], lhsT=threes[:], rhs=b_row[:], start=True, stop=True)
         quant_h(h_grp_s[:], R)
         quant_h(h_grp[:, 6:8], 6)
         regroup_w(0)
         quant_h(h_grp[:, 0:2], 0)
         regroup_w(1)
         quant_w(0)
+        banks = [new_bank(), new_bank()]
+        mx_pass(0, 0, banks[0])
+        mx_pass(1, 0, banks[1])
         regroup_w(2)
-        quant_w(1)
-        transposes(1)
-        transposes(2)
-        b_ps = psum.tile([P, C], F32, name="b_ps", tag="bank")
-        nc.tensor.matmul(b_ps[:], lhsT=threes[:], rhs=b_row[:], start=True, stop=True)
         nc.scalar.copy(out=bias[:], in_=b_ps[:])
+        quant_w(1)
+        copy_out(1, transposes(1))
         quant_w(2)
-        quant_h(h_grp[:, 2:4], 2)
-        banks = [passes(0), passes(1)]
+        mx_pass(0, 1, banks[0])
+        mx_pass(0, 2, banks[0])
+        mx_pass(1, 1, banks[1])
+        mx_pass(1, 2, banks[1])
+        copy_out(2, transposes(2))
         add_bias(0, banks[0])
-        quant_h(h_grp[:, 4:6], 4)
-        for r in range(2, R):
-            banks.append(passes(r))
+        quant_h(h_grp[:, 2:4], 2)
+        for r in range(2, 4):
+            banks.append(new_bank())
+            for j in range(TAPS):
+                mx_pass(r, j, banks[r])
         for r in range(R):
             if r + 1 < R:
                 add_bias(r + 1, banks[r + 1])
             row_max(r)
+            if r == 0:
+                quant_h(h_grp[:, 4:6], 4)
+                for t in range(4, R):
+                    banks.append(new_bank())
+                    for j in range(TAPS):
+                        mx_pass(t, j, banks[t])
             run_round(False)
             exp_sum(r)
             run_round(False)

@@ -28,7 +28,7 @@ LN_STEP = 1591.0 / 32768.0
 LN_C2 = -0.5
 LN_C3 = 0.3334271013736725
 LN_C4 = -0.25007814168930054
-LEVELS = 7
+FIRST_ON_VECTOR = 5
 
 
 def tile_predictor_pb_kernel(tc, H, W2, b2, out):
@@ -57,13 +57,12 @@ def tile_predictor_pb_kernel(tc, H, W2, b2, out):
         junk = keep.tile([P, C], BF16, name="junk")
         nm = keep.tile([P, R], F32, name="nm")
         s = keep.tile([P, R], F32, name="s")
-        consts = keep.tile([P, 4], F32, name="consts")
+        consts = keep.tile([P, 5], F32, name="consts")
         thr = keep.tile([P, N_THR], F32, name="thr")
         junk_t = keep.tile([P, N_THR], BF16, name="junk_t")
         cnt = keep.tile([P, R], F32, name="cnt")
-        ch = keep.tile([P, R, 8], F32, name="ch")
-        w = keep.tile([P, R], F32, name="w")
-        nl = keep.tile([P, R], F32, name="nl")
+        ch = keep.tile([P, R, 16], F32, name="ch")
+        nmb = keep.tile([P, R], F32, name="nmb")
         d = keep.tile([P, R], F32, name="d")
 
         nc.vector.memset(b_row[:], 0.0)
@@ -72,7 +71,7 @@ def tile_predictor_pb_kernel(tc, H, W2, b2, out):
         nc.vector.memset(consts[:, 0:1], -LN_STEP * N_THR / 2.0)
         nc.vector.memset(consts[:, 1:2], -1.0)
         nc.vector.memset(consts[:, 2:3], -LN_C3)
-        nc.vector.memset(consts[:, 3:4], -LN_C2)
+        nc.vector.memset(consts[:, 4:5], LN_C3 - LN_C2)
         nc.gpsimd.memset(thr[:, 0:1], EULER ** (LN_STEP / 2.0))
         for width in (1, 2, 4, 8, 16, 32, 64):
             nc.gpsimd.tensor_scalar(
@@ -91,10 +90,7 @@ def tile_predictor_pb_kernel(tc, H, W2, b2, out):
             nc.sync.dma_start(out=h_sb[:, 2 * a : 2 * a + 2, :], in_=h_view[:, 2 * a : 2 * a + 2, :])
 
         def load_w(j):
-            nc.sync.dma_start(
-                out=w_raw[:, j].rearrange("p (u e) c -> p u e c", u=2),
-                in_=W2[j].rearrange("(u q e) c -> q u e c", u=2, e=2),
-            )
+            nc.sync.dma_start(out=w_raw[:, j], in_=W2[j].rearrange("(p t) c -> p t c", t=4))
 
         load_h(3)
         load_h(0)
@@ -105,7 +101,7 @@ def tile_predictor_pb_kernel(tc, H, W2, b2, out):
         load_h(1)
         load_h(2)
 
-        h_words = h_sb[:].bitcast(F32).rearrange("m r (u p) -> m r u p", u=2)
+        h_words = h_sb[:].bitcast(F32).rearrange("m r (p u) -> m r u p", u=2)
         h_grp_w = h_grp[:].bitcast(F32)
         h_grp_s_w = h_grp_s[:].bitcast(F32)
 
@@ -123,12 +119,10 @@ def tile_predictor_pb_kernel(tc, H, W2, b2, out):
                     nc.tensor.transpose(
                         xt[:, r2, u, :], h_words[:, 2 * a + r2, u, :], ident[:]
                     )
-            return xt
-
-        def copy_out(a, xt):
             nc.scalar.copy(
                 out=h_grp_w[:, 2 * a : 2 * a + 2, :, :], in_=xt[:].rearrange("p r u m -> p r m u")
             )
+            return xt
 
         def regroup_w(j):
             for copy, c0, c1 in (
@@ -147,21 +141,20 @@ def tile_predictor_pb_kernel(tc, H, W2, b2, out):
                 in_=w_grp[:, j].rearrange("p c t -> p (c t)"),
             )
 
-        def mx_pass(r, j, z_ps):
-            src = r - (TAPS - 1 - j)
-            idx = src if src >= 0 else R + 2 + src
-            nc.tensor.matmul_mx(
-                out=z_ps[:],
-                lhsT=h_codes[:, idx, :].bitcast(FP8X4),
-                lhsT_scale=h_scales[:, idx, :],
-                rhs=w_codes[:, j, :].bitcast(FP8X4),
-                rhs_scale=w_scales[:, j, :],
-                start=(j == 0),
-                stop=(j == TAPS - 1),
-            )
-
-        def new_bank():
+        def passes(r):
             z_ps = psum.tile([P, C], F32, name="z_ps", tag="bank")
+            for j in range(TAPS):
+                src = r - (TAPS - 1 - j)
+                idx = src if src >= 0 else R + 2 + src
+                nc.tensor.matmul_mx(
+                    out=z_ps[:],
+                    lhsT=h_codes[:, idx, :].bitcast(FP8X4),
+                    lhsT_scale=h_scales[:, idx, :],
+                    rhs=w_codes[:, j, :].bitcast(FP8X4),
+                    rhs_scale=w_scales[:, j, :],
+                    start=(j == 0),
+                    stop=(j == TAPS - 1),
+                )
             return z_ps
 
         def add_bias(r, z_ps):
@@ -170,6 +163,14 @@ def tile_predictor_pb_kernel(tc, H, W2, b2, out):
         def row_max(r):
             nc.vector.tensor_reduce(
                 out=nm[:, r : r + 1], in_=z[:, r, :], axis=AX.X, op=ALU.max, negate=True
+            )
+            nc.gpsimd.tensor_scalar(
+                out=nmb[:, r : r + 1],
+                in0=nm[:, r : r + 1],
+                scalar1=1.0,
+                scalar2=1.0 - LN_STEP * N_THR / 2.0,
+                op0=ALU.mult,
+                op1=ALU.add,
             )
 
         def exp_sum(r):
@@ -185,10 +186,9 @@ def tile_predictor_pb_kernel(tc, H, W2, b2, out):
         def ident_act(dst, src, scale, bias):
             nc.scalar.activation(out=dst, in_=src, func=ACT.Identity, bias=bias, scale=scale)
 
-        def chain_level(r, k, on_vector):
+        def chain_level(r, k):
             one = slice(r, r + 1)
-            nl0 = nl[:, one]
-            e0, x, qa, qb, qc = [ch[:, r, i : i + 1] for i in range(5)]
+            w1, e0, x2, t1, t2, p1, p2, pad, ns, sc = [ch[:, r, i : i + 1] for i in range(10)]
             if k == 0:
                 nc.scalar.activation(
                     out=junk_t[:],
@@ -198,100 +198,83 @@ def tile_predictor_pb_kernel(tc, H, W2, b2, out):
                     scale=-1.0,
                     accum_out=cnt[:, one],
                 )
+                nc.scalar.activation(
+                    out=ch[:, r, 8:10], in_=consts[:, 1:3], func=ACT.Identity, scale=s[:, one]
+                )
             elif k == 1:
                 nc.scalar.activation(
                     out=e0, in_=cnt[:, one], func=ACT.Exp, bias=consts[:, 0:1], scale=-LN_STEP / 2.0
                 )
+                ident_act(w1, cnt[:, one], -LN_STEP / 2.0, nmb[:, one])
+            elif k == 2:
+                nc.scalar.activation(
+                    out=x2, in_=e0, func=ACT.Square, bias=consts[:, 1:2], scale=s[:, one]
+                )
+                ident_act(t2, e0, sc, consts[:, 4:5])
+                ident_act(t1, e0, ns, w1)
+            elif k == 3:
+                ident_act(p1, t2, x2, t1)
+                nc.scalar.activation(out=p2, in_=x2, func=ACT.Square, scale=(-LN_C4) ** 0.5)
+                if r >= FIRST_ON_VECTOR:
+                    nc.vector.tensor_scalar(
+                        out=z[:, r, :], in0=z[:, r, :], scalar1=p1, scalar2=p2, op0=ALU.add, op1=ALU.add
+                    )
+                    nc.sync.dma_start(out=out_view[:, r, :], in_=z[:, r, :])
+            else:
+                ident_act(d[:, one], p2, 1.0, p1)
                 nc.gpsimd.tensor_scalar(
-                    out=nl0,
-                    in0=cnt[:, one],
-                    scalar1=float(N_THR),
-                    scalar2=-LN_STEP / 2.0,
+                    out=z[:, r, :],
+                    in0=z[:, r, :],
+                    scalar1=d[:, one],
+                    scalar2=1.0,
                     op0=ALU.add,
                     op1=ALU.mult,
                 )
-                nc.gpsimd.tensor_tensor(out=w[:, one], in0=nm[:, one], in1=nl0, op=ALU.add)
-            elif k == 2:
-                ident_act(x, e0, s[:, one], consts[:, 1:2])
-            elif k == 3:
-                ident_act(qa, x, -LN_C4, consts[:, 2:3])
-            elif k == 4:
-                ident_act(qb, qa, x, consts[:, 3:4])
-            elif k == 5:
-                ident_act(qc, qb, x, consts[:, 1:2])
-            else:
-                ident_act(d[:, one], qc, x, w[:, one])
-                if on_vector:
-                    nc.vector.tensor_scalar(
-                        out=z[:, r, :], in0=z[:, r, :], scalar1=d[:, one], scalar2=None, op0=ALU.add
-                    )
-                else:
-                    nc.gpsimd.tensor_scalar(
-                        out=z[:, r, :],
-                        in0=z[:, r, :],
-                        scalar1=d[:, one],
-                        scalar2=1.0,
-                        op0=ALU.add,
-                        op1=ALU.mult,
-                    )
                 nc.sync.dma_start(out=out_view[:, r, :], in_=z[:, r, :])
 
+        levels = [4 if r >= FIRST_ON_VECTOR else 5 for r in range(R)]
         next_level = [0] * R
         started = []
 
-        def run_round(on_vector):
+        def run_round():
             for r in started:
-                if next_level[r] < LEVELS:
-                    chain_level(r, next_level[r], on_vector)
+                if next_level[r] < levels[r]:
+                    chain_level(r, next_level[r])
                     next_level[r] = next_level[r] + 1
 
         xt3 = transposes(3)
-        copy_out(3, xt3)
         nc.vector.tensor_copy(
             out=h_grp_s_w[:, :, 1:P, :],
             in_=xt3[:, :, :, 0 : P - 1].rearrange("p r u m -> p r m u"),
         )
-        copy_out(0, transposes(0))
-        b_ps = psum.tile([P, C], F32, name="b_ps", tag="bank")
-        nc.tensor.matmul(b_ps[:], lhsT=threes[:], rhs=b_row[:], start=True, stop=True)
+        transposes(0)
         quant_h(h_grp_s[:], R)
         quant_h(h_grp[:, 6:8], 6)
         regroup_w(0)
         quant_h(h_grp[:, 0:2], 0)
         regroup_w(1)
         quant_w(0)
-        banks = [new_bank(), new_bank()]
-        mx_pass(0, 0, banks[0])
-        mx_pass(1, 0, banks[1])
         regroup_w(2)
-        nc.scalar.copy(out=bias[:], in_=b_ps[:])
         quant_w(1)
-        copy_out(1, transposes(1))
+        transposes(1)
+        transposes(2)
+        b_ps = psum.tile([P, C], F32, name="b_ps", tag="bank")
+        nc.tensor.matmul(b_ps[:], lhsT=threes[:], rhs=b_row[:], start=True, stop=True)
+        nc.scalar.copy(out=bias[:], in_=b_ps[:])
         quant_w(2)
-        mx_pass(0, 1, banks[0])
-        mx_pass(0, 2, banks[0])
-        mx_pass(1, 1, banks[1])
-        mx_pass(1, 2, banks[1])
-        copy_out(2, transposes(2))
-        add_bias(0, banks[0])
         quant_h(h_grp[:, 2:4], 2)
-        for r in range(2, 4):
-            banks.append(new_bank())
-            for j in range(TAPS):
-                mx_pass(r, j, banks[r])
+        banks = [passes(0), passes(1)]
+        add_bias(0, banks[0])
+        quant_h(h_grp[:, 4:6], 4)
+        for r in range(2, R):
+            banks.append(passes(r))
         for r in range(R):
             if r + 1 < R:
                 add_bias(r + 1, banks[r + 1])
             row_max(r)
-            if r == 0:
-                quant_h(h_grp[:, 4:6], 4)
-                for t in range(4, R):
-                    banks.append(new_bank())
-                    for j in range(TAPS):
-                        mx_pass(t, j, banks[t])
-            run_round(False)
+            run_round()
             exp_sum(r)
-            run_round(False)
+            run_round()
             started.append(r)
-        for k in range(LEVELS):
-            run_round(True)
+        for k in range(4):
+            run_round()

@@ -13,11 +13,12 @@ ACT = mybir.ActivationFunctionType
 AX = mybir.AxisListType
 
 P = 128
+PACK = 4
 ROWS = 1024
 K = 512
 C = 512
 TAPS = 3
-R = 8
+R = ROWS // P
 FLOPS = 2 * ROWS * K * C * TAPS
 
 V_COLS = 256
@@ -28,7 +29,24 @@ LN_STEP = 1591.0 / 32768.0
 LN_C2 = -0.5
 LN_C3 = 0.3334271013736725
 LN_C4 = -0.25007814168930054
+LN_LEVELS = 4
 FIRST_ON_VECTOR = 5
+
+K_GUESS = 0
+K_MINUS_ONE = 1
+K_MINUS_C3 = 2
+K_T2 = 3
+N_CONSTS = 4
+L_W1 = 0
+L_E0 = 1
+L_X2 = 2
+L_T1 = 3
+L_T2 = 4
+L_P1 = 5
+L_P2 = 6
+L_NEG_S = 7
+L_C3_S = 8
+N_LN_COLS = 9
 
 
 def tile_predictor_pb_kernel(tc, H, W2, b2, out):
@@ -39,44 +57,43 @@ def tile_predictor_pb_kernel(tc, H, W2, b2, out):
         ctx.enter_context(tc.manual_schedule())
 
         ident = keep.tile([P, P], F32, name="ident")
-        make_identity(nc, ident[:])
-
         h_sb = keep.tile([P, R, K], BF16, name="h_sb")
-        w_raw = keep.tile([P, TAPS, 4, C], BF16, name="w_raw")
+        w_raw = keep.tile([P, TAPS, PACK, C], BF16, name="w_raw")
         b_row = keep.tile([P, C], BF16, name="b_row")
         threes = keep.tile([P, P], BF16, name="threes")
         bias = keep.tile([P, C], F32, name="bias")
-        h_grp = keep.tile([P, R, P, 4], BF16, name="h_grp", align_bytes=64)
-        h_grp_s = keep.tile([P, 2, P, 4], BF16, name="h_grp_s", align_bytes=64)
-        w_grp = keep.tile([P, TAPS, C, 4], BF16, name="w_grp", align_bytes=64)
+        h_grp = keep.tile([P, R, P, PACK], BF16, name="h_grp", align_bytes=64)
+        h_grp_moved = keep.tile([P, 2, P, PACK], BF16, name="h_grp_moved", align_bytes=64)
+        w_grp = keep.tile([P, TAPS, C, PACK], BF16, name="w_grp", align_bytes=64)
         h_codes = keep.tile([P, R + 2, P], U32, name="h_codes", align_bytes=64)
         h_scales = keep.tile([P, R + 2, P], U8, name="h_scales", align_bytes=64)
         w_codes = keep.tile([P, TAPS, C], U32, name="w_codes", align_bytes=64)
         w_scales = keep.tile([P, TAPS, C], U8, name="w_scales", align_bytes=64)
         z = keep.tile([P, R, C], F32, name="z")
-        junk = keep.tile([P, C], BF16, name="junk")
-        nm = keep.tile([P, R], F32, name="nm")
-        s = keep.tile([P, R], F32, name="s")
-        consts = keep.tile([P, 5], F32, name="consts")
-        thr = keep.tile([P, N_THR], F32, name="thr")
-        junk_t = keep.tile([P, N_THR], BF16, name="junk_t")
-        cnt = keep.tile([P, R], F32, name="cnt")
-        ch = keep.tile([P, R, 16], F32, name="ch")
-        nmb = keep.tile([P, R], F32, name="nmb")
-        d = keep.tile([P, R], F32, name="d")
+        exp_out = keep.tile([P, C], BF16, name="exp_out")
+        sign_out = keep.tile([P, N_THR], BF16, name="sign_out")
+        neg_max = keep.tile([P, R], F32, name="neg_max")
+        neg_max_c = keep.tile([P, R], F32, name="neg_max_c")
+        thresholds = keep.tile([P, N_THR], F32, name="thresholds")
+        consts = keep.tile([P, N_CONSTS], F32, name="consts")
+        row_sum = keep.tile([P, R], F32, name="row_sum")
+        count = keep.tile([P, R], F32, name="count")
+        shift = keep.tile([P, R], F32, name="shift")
+        ln_row = keep.tile([P, R, N_LN_COLS], F32, name="ln_row")
 
+        make_identity(nc, ident[:])
         nc.vector.memset(b_row[:], 0.0)
         nc.vector.memset(threes[:], 3.0)
-        nc.vector.memset(h_grp_s[:], 0.0)
-        nc.vector.memset(consts[:, 0:1], -LN_STEP * N_THR / 2.0)
-        nc.vector.memset(consts[:, 1:2], -1.0)
-        nc.vector.memset(consts[:, 2:3], -LN_C3)
-        nc.vector.memset(consts[:, 4:5], LN_C3 - LN_C2)
-        nc.gpsimd.memset(thr[:, 0:1], EULER ** (LN_STEP / 2.0))
+        nc.vector.memset(h_grp_moved[:], 0.0)
+        nc.vector.memset(consts[:, K_GUESS : K_GUESS + 1], -LN_STEP * N_THR / 2.0)
+        nc.vector.memset(consts[:, K_MINUS_ONE : K_MINUS_ONE + 1], -1.0)
+        nc.vector.memset(consts[:, K_MINUS_C3 : K_MINUS_C3 + 1], -LN_C3)
+        nc.vector.memset(consts[:, K_T2 : K_T2 + 1], LN_C3 - LN_C2)
+        nc.gpsimd.memset(thresholds[:, 0:1], EULER ** (LN_STEP / 2.0))
         for width in (1, 2, 4, 8, 16, 32, 64):
             nc.gpsimd.tensor_scalar(
-                out=thr[:, width : 2 * width],
-                in0=thr[:, 0:width],
+                out=thresholds[:, width : 2 * width],
+                in0=thresholds[:, 0:width],
                 scalar1=EULER ** (LN_STEP * width),
                 scalar2=0.0,
                 op0=ALU.mult,
@@ -86,195 +103,211 @@ def tile_predictor_pb_kernel(tc, H, W2, b2, out):
         h_view = H.rearrange("(m r) k -> m r k", r=R)
         out_view = out.rearrange("(m r) c -> m r c", r=R)
 
-        def load_h(a):
-            nc.sync.dma_start(out=h_sb[:, 2 * a : 2 * a + 2, :], in_=h_view[:, 2 * a : 2 * a + 2, :])
+        def load_h_pair(a):
+            pair = slice(2 * a, 2 * a + 2)
+            nc.sync.dma_start(out=h_sb[:, pair, :], in_=h_view[:, pair, :])
 
         def load_w(j):
-            nc.sync.dma_start(out=w_raw[:, j], in_=W2[j].rearrange("(p t) c -> p t c", t=4))
+            nc.sync.dma_start(out=w_raw[:, j], in_=W2[j].rearrange("(p t) c -> p t c", t=PACK))
 
-        load_h(3)
-        load_h(0)
+        load_h_pair(3)
+        load_h_pair(0)
         nc.sync.dma_start(out=b_row[0:1, :], in_=b2)
         load_w(0)
         load_w(1)
         load_w(2)
-        load_h(1)
-        load_h(2)
+        load_h_pair(1)
+        load_h_pair(2)
 
         h_words = h_sb[:].bitcast(F32).rearrange("m r (p u) -> m r u p", u=2)
-        h_grp_w = h_grp[:].bitcast(F32)
-        h_grp_s_w = h_grp_s[:].bitcast(F32)
+        h_grp_words = h_grp[:].bitcast(F32)
+        h_grp_moved_words = h_grp_moved[:].bitcast(F32)
 
-        def quant_h(src, t0):
-            nc.vector.quantize_mx(
-                out=h_codes[:, t0 : t0 + 2, :].rearrange("p r m -> p (r m)").bitcast(FP8X4),
-                scales=h_scales[:, t0 : t0 + 2, :].rearrange("p r m -> p (r m)"),
-                in_=src.rearrange("p r m t -> p (r m t)"),
-            )
-
-        def transposes(a):
-            xt = psum.tile([P, 2, 2, P], F32, name="xt", tag="bank")
-            for r2 in range(2):
+        def transpose_pair(a):
+            flipped = psum.tile([P, 2, 2, P], F32, name="flipped", tag="bank")
+            for i in range(2):
                 for u in range(2):
-                    nc.tensor.transpose(
-                        xt[:, r2, u, :], h_words[:, 2 * a + r2, u, :], ident[:]
-                    )
+                    nc.tensor.transpose(flipped[:, i, u, :], h_words[:, 2 * a + i, u, :], ident[:])
             nc.scalar.copy(
-                out=h_grp_w[:, 2 * a : 2 * a + 2, :, :], in_=xt[:].rearrange("p r u m -> p r m u")
+                out=h_grp_words[:, 2 * a : 2 * a + 2, :, :],
+                in_=flipped[:].rearrange("p i u m -> p i m u"),
             )
-            return xt
+            return flipped
+
+        def quantise_h(grouped, first):
+            nc.vector.quantize_mx(
+                out=h_codes[:, first : first + 2, :].rearrange("p i m -> p (i m)").bitcast(FP8X4),
+                scales=h_scales[:, first : first + 2, :].rearrange("p i m -> p (i m)"),
+                in_=grouped.rearrange("p i m t -> p (i m t)"),
+            )
+
+        def quantise_h_pair(a):
+            quantise_h(h_grp[:, 2 * a : 2 * a + 2], 2 * a)
 
         def regroup_w(j):
-            for copy, c0, c1 in (
-                (nc.vector.tensor_copy, 0, V_COLS),
-                (nc.scalar.copy, V_COLS, C),
-            ):
+            for copy, c0, c1 in ((nc.vector.tensor_copy, 0, V_COLS), (nc.scalar.copy, V_COLS, C)):
                 copy(
                     out=w_grp[:, j, c0:c1, :].rearrange("p (c i) t -> p c t i", i=4),
                     in_=w_raw[:, j, :, c0:c1].rearrange("p t (c i) -> p c t i", i=4),
                 )
 
-        def quant_w(j):
+        def quantise_w(j):
             nc.vector.quantize_mx(
                 out=w_codes[:, j, :].bitcast(FP8X4),
                 scales=w_scales[:, j, :],
                 in_=w_grp[:, j].rearrange("p c t -> p (c t)"),
             )
 
-        def passes(r):
-            z_ps = psum.tile([P, C], F32, name="z_ps", tag="bank")
+        def multiply(r):
+            acc = psum.tile([P, C], F32, name="acc", tag="bank")
             for j in range(TAPS):
-                src = r - (TAPS - 1 - j)
-                idx = src if src >= 0 else R + 2 + src
+                source = r - (TAPS - 1 - j)
+                if source < 0:
+                    source = R + 2 + source
                 nc.tensor.matmul_mx(
-                    out=z_ps[:],
-                    lhsT=h_codes[:, idx, :].bitcast(FP8X4),
-                    lhsT_scale=h_scales[:, idx, :],
+                    out=acc[:],
+                    lhsT=h_codes[:, source, :].bitcast(FP8X4),
+                    lhsT_scale=h_scales[:, source, :],
                     rhs=w_codes[:, j, :].bitcast(FP8X4),
                     rhs_scale=w_scales[:, j, :],
                     start=(j == 0),
                     stop=(j == TAPS - 1),
                 )
-            return z_ps
+            return acc
 
-        def add_bias(r, z_ps):
-            nc.vector.tensor_tensor(out=z[:, r, :], in0=z_ps[:], in1=bias[:], op=ALU.add)
+        def add_bias(r, acc):
+            nc.vector.tensor_tensor(out=z[:, r, :], in0=acc[:], in1=bias[:], op=ALU.add)
 
         def row_max(r):
+            one = slice(r, r + 1)
             nc.vector.tensor_reduce(
-                out=nm[:, r : r + 1], in_=z[:, r, :], axis=AX.X, op=ALU.max, negate=True
+                out=neg_max[:, one], in_=z[:, r, :], axis=AX.X, op=ALU.max, negate=True
             )
             nc.gpsimd.tensor_scalar(
-                out=nmb[:, r : r + 1],
-                in0=nm[:, r : r + 1],
+                out=neg_max_c[:, one],
+                in0=neg_max[:, one],
                 scalar1=1.0,
                 scalar2=1.0 - LN_STEP * N_THR / 2.0,
                 op0=ALU.mult,
                 op1=ALU.add,
             )
 
-        def exp_sum(r):
+        def exp_and_sum(r):
+            one = slice(r, r + 1)
             nc.scalar.activation(
-                out=junk[:],
+                out=exp_out[:],
                 in_=z[:, r, :],
                 func=ACT.Exp,
-                bias=nm[:, r : r + 1],
+                bias=neg_max[:, one],
                 scale=1.0,
-                accum_out=s[:, r : r + 1],
+                accum_out=row_sum[:, one],
             )
 
-        def ident_act(dst, src, scale, bias):
-            nc.scalar.activation(out=dst, in_=src, func=ACT.Identity, bias=bias, scale=scale)
-
-        def chain_level(r, k):
+        def ln_level(r, level):
             one = slice(r, r + 1)
-            w1, e0, x2, t1, t2, p1, p2, pad, ns, sc = [ch[:, r, i : i + 1] for i in range(10)]
-            if k == 0:
+            s = row_sum[:, one]
+
+            def col(i):
+                return ln_row[:, r, i : i + 1]
+
+            def const(i):
+                return consts[:, i : i + 1]
+
+            def act(func, dst, src, scale, offset):
+                nc.scalar.activation(out=dst, in_=src, func=func, bias=offset, scale=scale)
+
+            if level == 0:
                 nc.scalar.activation(
-                    out=junk_t[:],
-                    in_=thr[:],
+                    out=sign_out[:],
+                    in_=thresholds[:],
                     func=ACT.Sign,
-                    bias=s[:, one],
+                    bias=s,
                     scale=-1.0,
-                    accum_out=cnt[:, one],
+                    accum_out=count[:, one],
                 )
                 nc.scalar.activation(
-                    out=ch[:, r, 8:10], in_=consts[:, 1:3], func=ACT.Identity, scale=s[:, one]
+                    out=ln_row[:, r, L_NEG_S : L_C3_S + 1],
+                    in_=consts[:, K_MINUS_ONE : K_MINUS_C3 + 1],
+                    func=ACT.Identity,
+                    scale=s,
                 )
-            elif k == 1:
+            elif level == 1:
+                act(ACT.Exp, col(L_E0), count[:, one], -LN_STEP / 2.0, const(K_GUESS))
+                act(ACT.Identity, col(L_W1), count[:, one], -LN_STEP / 2.0, neg_max_c[:, one])
+            elif level == 2:
+                act(ACT.Square, col(L_X2), col(L_E0), s, const(K_MINUS_ONE))
+                act(ACT.Identity, col(L_T2), col(L_E0), col(L_C3_S), const(K_T2))
+                act(ACT.Identity, col(L_T1), col(L_E0), col(L_NEG_S), col(L_W1))
+            elif level == 3:
+                act(ACT.Identity, col(L_P1), col(L_T2), col(L_X2), col(L_T1))
                 nc.scalar.activation(
-                    out=e0, in_=cnt[:, one], func=ACT.Exp, bias=consts[:, 0:1], scale=-LN_STEP / 2.0
+                    out=col(L_P2), in_=col(L_X2), func=ACT.Square, scale=(-LN_C4) ** 0.5
                 )
-                ident_act(w1, cnt[:, one], -LN_STEP / 2.0, nmb[:, one])
-            elif k == 2:
-                nc.scalar.activation(
-                    out=x2, in_=e0, func=ACT.Square, bias=consts[:, 1:2], scale=s[:, one]
-                )
-                ident_act(t2, e0, sc, consts[:, 4:5])
-                ident_act(t1, e0, ns, w1)
-            elif k == 3:
-                ident_act(p1, t2, x2, t1)
-                nc.scalar.activation(out=p2, in_=x2, func=ACT.Square, scale=(-LN_C4) ** 0.5)
                 if r >= FIRST_ON_VECTOR:
                     nc.vector.tensor_scalar(
-                        out=z[:, r, :], in0=z[:, r, :], scalar1=p1, scalar2=p2, op0=ALU.add, op1=ALU.add
+                        out=z[:, r, :],
+                        in0=z[:, r, :],
+                        scalar1=col(L_P1),
+                        scalar2=col(L_P2),
+                        op0=ALU.add,
+                        op1=ALU.add,
                     )
                     nc.sync.dma_start(out=out_view[:, r, :], in_=z[:, r, :])
             else:
-                ident_act(d[:, one], p2, 1.0, p1)
+                act(ACT.Identity, shift[:, one], col(L_P2), 1.0, col(L_P1))
                 nc.gpsimd.tensor_scalar(
                     out=z[:, r, :],
                     in0=z[:, r, :],
-                    scalar1=d[:, one],
+                    scalar1=shift[:, one],
                     scalar2=1.0,
                     op0=ALU.add,
                     op1=ALU.mult,
                 )
                 nc.sync.dma_start(out=out_view[:, r, :], in_=z[:, r, :])
 
-        levels = [4 if r >= FIRST_ON_VECTOR else 5 for r in range(R)]
+        levels = [LN_LEVELS if r >= FIRST_ON_VECTOR else LN_LEVELS + 1 for r in range(R)]
         next_level = [0] * R
-        started = []
+        summed = []
 
-        def run_round():
-            for r in started:
+        def ln_round():
+            for r in summed:
                 if next_level[r] < levels[r]:
-                    chain_level(r, next_level[r])
+                    ln_level(r, next_level[r])
                     next_level[r] = next_level[r] + 1
 
-        xt3 = transposes(3)
+        flipped_67 = transpose_pair(3)
         nc.vector.tensor_copy(
-            out=h_grp_s_w[:, :, 1:P, :],
-            in_=xt3[:, :, :, 0 : P - 1].rearrange("p r u m -> p r m u"),
+            out=h_grp_moved_words[:, :, 1:P, :],
+            in_=flipped_67[:, :, :, 0 : P - 1].rearrange("p i u m -> p i m u"),
         )
-        transposes(0)
-        quant_h(h_grp_s[:], R)
-        quant_h(h_grp[:, 6:8], 6)
+        transpose_pair(0)
+        bias_ps = psum.tile([P, C], F32, name="bias_ps", tag="bank")
+        nc.tensor.matmul(bias_ps[:], lhsT=threes[:], rhs=b_row[:], start=True, stop=True)
+        quantise_h_pair(3)
+        quantise_h(h_grp_moved[:], R)
         regroup_w(0)
-        quant_h(h_grp[:, 0:2], 0)
+        quantise_h_pair(0)
         regroup_w(1)
-        quant_w(0)
+        quantise_w(0)
         regroup_w(2)
-        quant_w(1)
-        transposes(1)
-        transposes(2)
-        b_ps = psum.tile([P, C], F32, name="b_ps", tag="bank")
-        nc.tensor.matmul(b_ps[:], lhsT=threes[:], rhs=b_row[:], start=True, stop=True)
-        nc.scalar.copy(out=bias[:], in_=b_ps[:])
-        quant_w(2)
-        quant_h(h_grp[:, 2:4], 2)
-        banks = [passes(0), passes(1)]
-        add_bias(0, banks[0])
-        quant_h(h_grp[:, 4:6], 4)
+        nc.scalar.copy(out=bias[:], in_=bias_ps[:])
+        quantise_w(1)
+        transpose_pair(1)
+        transpose_pair(2)
+        quantise_w(2)
+        quantise_h_pair(1)
+        accs = [multiply(0), multiply(1)]
+        add_bias(0, accs[0])
+        quantise_h_pair(2)
         for r in range(2, R):
-            banks.append(passes(r))
+            accs.append(multiply(r))
         for r in range(R):
             if r + 1 < R:
-                add_bias(r + 1, banks[r + 1])
+                add_bias(r + 1, accs[r + 1])
             row_max(r)
-            run_round()
-            exp_sum(r)
-            run_round()
-            started.append(r)
-        for k in range(4):
-            run_round()
+            ln_round()
+            exp_and_sum(r)
+            ln_round()
+            summed.append(r)
+        for level in range(LN_LEVELS):
+            ln_round()

@@ -26,27 +26,25 @@ V_COLS = 256
 EULER = 2.718281828459045
 N_THR = 128
 LN_STEP = 1591.0 / 32768.0
-LN_C2 = -0.5
-LN_C3 = 0.3334271013736725
-LN_C4 = -0.25007814168930054
-LN_LEVELS = 4
+LN_C0 = -0.2498800083345607
+LN_C1 = 0.49992698431015015
+LN_BETA = 0.6138098239898682
+LN_ALPHA = 1.9999163150787354
+LN_LEVELS = 3
 FIRST_ON_VECTOR = 5
 
 K_GUESS = 0
-K_MINUS_ONE = 1
-K_MINUS_C3 = 2
-K_T2 = 3
+K_C1 = 1
+K_MINUS_ALPHA = 2
+K_BETA = 3
 N_CONSTS = 4
-L_W1 = 0
-L_E0 = 1
-L_X2 = 2
-L_T1 = 3
-L_T2 = 4
-L_P1 = 5
-L_P2 = 6
-L_NEG_S = 7
-L_C3_S = 8
-N_LN_COLS = 9
+L_E0 = 0
+L_Q = 1
+L_T = 2
+L_B = 3
+L_C1_S = 4
+L_ALPHA_S = 5
+N_LN_COLS = 6
 
 
 def tile_predictor_pb_kernel(tc, H, W2, b2, out):
@@ -86,9 +84,9 @@ def tile_predictor_pb_kernel(tc, H, W2, b2, out):
         nc.vector.memset(threes[:], 3.0)
         nc.vector.memset(h_grp_moved[:], 0.0)
         nc.vector.memset(consts[:, K_GUESS : K_GUESS + 1], -LN_STEP * N_THR / 2.0)
-        nc.vector.memset(consts[:, K_MINUS_ONE : K_MINUS_ONE + 1], -1.0)
-        nc.vector.memset(consts[:, K_MINUS_C3 : K_MINUS_C3 + 1], -LN_C3)
-        nc.vector.memset(consts[:, K_T2 : K_T2 + 1], LN_C3 - LN_C2)
+        nc.vector.memset(consts[:, K_C1 : K_C1 + 1], LN_C1)
+        nc.vector.memset(consts[:, K_MINUS_ALPHA : K_MINUS_ALPHA + 1], -LN_ALPHA)
+        nc.vector.memset(consts[:, K_BETA : K_BETA + 1], LN_BETA)
         nc.gpsimd.memset(thresholds[:, 0:1], EULER ** (LN_STEP / 2.0))
         for width in (1, 2, 4, 8, 16, 32, 64):
             nc.gpsimd.tensor_scalar(
@@ -186,8 +184,8 @@ def tile_predictor_pb_kernel(tc, H, W2, b2, out):
             nc.gpsimd.tensor_scalar(
                 out=neg_max_c[:, one],
                 in0=neg_max[:, one],
-                scalar1=1.0,
-                scalar2=1.0 - LN_STEP * N_THR / 2.0,
+                scalar1=-1.0,
+                scalar2=LN_STEP * N_THR / 2.0 + LN_C0,
                 op0=ALU.mult,
                 op1=ALU.add,
             )
@@ -226,35 +224,30 @@ def tile_predictor_pb_kernel(tc, H, W2, b2, out):
                     accum_out=count[:, one],
                 )
                 nc.scalar.activation(
-                    out=ln_row[:, r, L_NEG_S : L_C3_S + 1],
-                    in_=consts[:, K_MINUS_ONE : K_MINUS_C3 + 1],
+                    out=ln_row[:, r, L_C1_S : L_ALPHA_S + 1],
+                    in_=consts[:, K_C1 : K_MINUS_ALPHA + 1],
                     func=ACT.Identity,
                     scale=s,
                 )
             elif level == 1:
                 act(ACT.Exp, col(L_E0), count[:, one], -LN_STEP / 2.0, const(K_GUESS))
-                act(ACT.Identity, col(L_W1), count[:, one], -LN_STEP / 2.0, neg_max_c[:, one])
+                act(ACT.Identity, col(L_Q), count[:, one], LN_STEP / 2.0, neg_max_c[:, one])
             elif level == 2:
-                act(ACT.Square, col(L_X2), col(L_E0), s, const(K_MINUS_ONE))
-                act(ACT.Identity, col(L_T2), col(L_E0), col(L_C3_S), const(K_T2))
-                act(ACT.Identity, col(L_T1), col(L_E0), col(L_NEG_S), col(L_W1))
-            elif level == 3:
-                act(ACT.Identity, col(L_P1), col(L_T2), col(L_X2), col(L_T1))
-                nc.scalar.activation(
-                    out=col(L_P2), in_=col(L_X2), func=ACT.Square, scale=(-LN_C4) ** 0.5
-                )
+                act(ACT.Identity, col(L_T), col(L_E0), col(L_C1_S), col(L_Q))
+                act(ACT.Exp, col(L_B), col(L_E0), col(L_ALPHA_S), const(K_BETA))
                 if r >= FIRST_ON_VECTOR:
                     nc.vector.tensor_scalar(
                         out=z[:, r, :],
                         in0=z[:, r, :],
-                        scalar1=col(L_P1),
-                        scalar2=col(L_P2),
-                        op0=ALU.add,
+                        scalar1=col(L_T),
+                        scalar2=col(L_B),
+                        op0=ALU.subtract,
                         op1=ALU.add,
                     )
                     nc.sync.dma_start(out=out_view[:, r, :], in_=z[:, r, :])
+            elif level == 3:
+                act(ACT.Identity, shift[:, one], col(L_T), -1.0, col(L_B))
             else:
-                act(ACT.Identity, shift[:, one], col(L_P2), 1.0, col(L_P1))
                 nc.gpsimd.tensor_scalar(
                     out=z[:, r, :],
                     in0=z[:, r, :],
@@ -265,12 +258,12 @@ def tile_predictor_pb_kernel(tc, H, W2, b2, out):
                 )
                 nc.sync.dma_start(out=out_view[:, r, :], in_=z[:, r, :])
 
-        levels = [LN_LEVELS if r >= FIRST_ON_VECTOR else LN_LEVELS + 1 for r in range(R)]
+        levels = [LN_LEVELS if r >= FIRST_ON_VECTOR else LN_LEVELS + 2 for r in range(R)]
         next_level = [0] * R
         summed = []
 
         def ln_round():
-            for r in summed:
+            for r in reversed(summed):
                 if next_level[r] < levels[r]:
                     ln_level(r, next_level[r])
                     next_level[r] = next_level[r] + 1

@@ -7,6 +7,7 @@ F32 = mybir.dt.float32
 BF16 = mybir.dt.bfloat16
 U32 = mybir.dt.uint32
 U8 = mybir.dt.uint8
+I32 = mybir.dt.int32
 FP8X4 = mybir.dt.float8_e4m3fn_x4
 ALU = mybir.AluOpType
 ACT = mybir.ActivationFunctionType
@@ -21,7 +22,7 @@ TAPS = 3
 R = ROWS // P
 FLOPS = 2 * ROWS * K * C * TAPS
 
-V_COLS = 256
+V_COLS = 320
 
 EULER = 2.718281828459045
 N_THR = 128
@@ -31,7 +32,8 @@ LN_C1 = 0.49992698431015015
 LN_BETA = 0.6138098239898682
 LN_ALPHA = 1.9999163150787354
 LN_LEVELS = 3
-FIRST_ON_VECTOR = 5
+SEQ = (2, 3, 4, 5, 6, 7, 0, 1)
+ON_VECTOR = SEQ[5:]
 
 K_GUESS = 0
 K_C1 = 1
@@ -61,7 +63,6 @@ def tile_predictor_pb_kernel(tc, H, W2, b2, out):
         threes = keep.tile([P, P], BF16, name="threes")
         bias = keep.tile([P, C], F32, name="bias")
         h_grp = keep.tile([P, R, P, PACK], BF16, name="h_grp", align_bytes=64)
-        h_grp_moved = keep.tile([P, 2, P, PACK], BF16, name="h_grp_moved", align_bytes=64)
         w_grp = keep.tile([P, TAPS, C, PACK], BF16, name="w_grp", align_bytes=64)
         h_codes = keep.tile([P, R + 2, P], U32, name="h_codes", align_bytes=64)
         h_scales = keep.tile([P, R + 2, P], U8, name="h_scales", align_bytes=64)
@@ -82,7 +83,8 @@ def tile_predictor_pb_kernel(tc, H, W2, b2, out):
         make_identity(nc, ident[:])
         nc.vector.memset(b_row[:], 0.0)
         nc.vector.memset(threes[:], 3.0)
-        nc.vector.memset(h_grp_moved[:], 0.0)
+        nc.vector.memset(h_codes[:, R : R + 2, :].bitcast(I32), 0)
+        nc.vector.memset(h_scales[:].bitcast(I32), 0)
         nc.vector.memset(consts[:, K_GUESS : K_GUESS + 1], -LN_STEP * N_THR / 2.0)
         nc.vector.memset(consts[:, K_C1 : K_C1 + 1], LN_C1)
         nc.vector.memset(consts[:, K_MINUS_ALPHA : K_MINUS_ALPHA + 1], -LN_ALPHA)
@@ -108,18 +110,17 @@ def tile_predictor_pb_kernel(tc, H, W2, b2, out):
         def load_w(j):
             nc.sync.dma_start(out=w_raw[:, j], in_=W2[j].rearrange("(p t) c -> p t c", t=PACK))
 
-        load_h_pair(3)
-        load_h_pair(0)
-        nc.sync.dma_start(out=b_row[0:1, :], in_=b2)
         load_w(0)
+        load_h_pair(0)
+        load_h_pair(1)
+        nc.sync.dma_start(out=b_row[0:1, :], in_=b2)
         load_w(1)
         load_w(2)
-        load_h_pair(1)
         load_h_pair(2)
+        load_h_pair(3)
 
         h_words = h_sb[:].bitcast(F32).rearrange("m r (p u) -> m r u p", u=2)
         h_grp_words = h_grp[:].bitcast(F32)
-        h_grp_moved_words = h_grp_moved[:].bitcast(F32)
 
         def transpose_pair(a):
             flipped = psum.tile([P, 2, 2, P], F32, name="flipped", tag="bank")
@@ -156,21 +157,28 @@ def tile_predictor_pb_kernel(tc, H, W2, b2, out):
                 in_=w_grp[:, j].rearrange("p c t -> p (c t)"),
             )
 
-        def multiply(r):
+        def new_acc():
             acc = psum.tile([P, C], F32, name="acc", tag="bank")
+            return acc
+
+        def tap_pass(r, j, acc):
+            source = r - (TAPS - 1 - j)
+            if source < 0:
+                source = R + 2 + source
+            nc.tensor.matmul_mx(
+                out=acc[:],
+                lhsT=h_codes[:, source, :].bitcast(FP8X4),
+                lhsT_scale=h_scales[:, source, :],
+                rhs=w_codes[:, j, :].bitcast(FP8X4),
+                rhs_scale=w_scales[:, j, :],
+                start=(j == 0),
+                stop=(j == TAPS - 1),
+            )
+
+        def multiply(r):
+            acc = new_acc()
             for j in range(TAPS):
-                source = r - (TAPS - 1 - j)
-                if source < 0:
-                    source = R + 2 + source
-                nc.tensor.matmul_mx(
-                    out=acc[:],
-                    lhsT=h_codes[:, source, :].bitcast(FP8X4),
-                    lhsT_scale=h_scales[:, source, :],
-                    rhs=w_codes[:, j, :].bitcast(FP8X4),
-                    rhs_scale=w_scales[:, j, :],
-                    start=(j == 0),
-                    stop=(j == TAPS - 1),
-                )
+                tap_pass(r, j, acc)
             return acc
 
         def add_bias(r, acc):
@@ -235,7 +243,7 @@ def tile_predictor_pb_kernel(tc, H, W2, b2, out):
             elif level == 2:
                 act(ACT.Identity, col(L_T), col(L_E0), col(L_C1_S), col(L_Q))
                 act(ACT.Exp, col(L_B), col(L_E0), col(L_ALPHA_S), const(K_BETA))
-                if r >= FIRST_ON_VECTOR:
+                if r in ON_VECTOR:
                     nc.vector.tensor_scalar(
                         out=z[:, r, :],
                         in0=z[:, r, :],
@@ -258,7 +266,7 @@ def tile_predictor_pb_kernel(tc, H, W2, b2, out):
                 )
                 nc.sync.dma_start(out=out_view[:, r, :], in_=z[:, r, :])
 
-        levels = [LN_LEVELS if r >= FIRST_ON_VECTOR else LN_LEVELS + 2 for r in range(R)]
+        levels = [LN_LEVELS if r in ON_VECTOR else LN_LEVELS + 2 for r in range(R)]
         next_level = [0] * R
         summed = []
 
@@ -268,36 +276,49 @@ def tile_predictor_pb_kernel(tc, H, W2, b2, out):
                     ln_level(r, next_level[r])
                     next_level[r] = next_level[r] + 1
 
-        flipped_67 = transpose_pair(3)
-        nc.vector.tensor_copy(
-            out=h_grp_moved_words[:, :, 1:P, :],
-            in_=flipped_67[:, :, :, 0 : P - 1].rearrange("p i u m -> p i m u"),
-        )
+        regroup_w(0)
         transpose_pair(0)
+        quantise_w(0)
+        regroup_w(1)
+        quantise_h_pair(0)
+        transpose_pair(1)
         bias_ps = psum.tile([P, C], F32, name="bias_ps", tag="bank")
         nc.tensor.matmul(bias_ps[:], lhsT=threes[:], rhs=b_row[:], start=True, stop=True)
-        quantise_h_pair(3)
-        quantise_h(h_grp_moved[:], R)
-        regroup_w(0)
-        quantise_h_pair(0)
-        regroup_w(1)
-        quantise_w(0)
-        regroup_w(2)
-        nc.scalar.copy(out=bias[:], in_=bias_ps[:])
         quantise_w(1)
-        transpose_pair(1)
-        transpose_pair(2)
-        quantise_w(2)
+        accs = {}
+        accs[2] = new_acc()
+        accs[3] = new_acc()
+        tap_pass(2, 0, accs[2])
+        tap_pass(3, 0, accs[3])
+        tap_pass(2, 1, accs[2])
+        regroup_w(2)
         quantise_h_pair(1)
-        accs = [multiply(0), multiply(1)]
-        add_bias(0, accs[0])
+        nc.scalar.copy(out=bias[:], in_=bias_ps[:])
+        quantise_w(2)
+        transpose_pair(2)
+        transpose_pair(3)
+        tap_pass(3, 1, accs[3])
+        tap_pass(2, 2, accs[2])
+        tap_pass(3, 2, accs[3])
         quantise_h_pair(2)
-        for r in range(2, R):
-            accs.append(multiply(r))
-        for r in range(R):
-            if r + 1 < R:
-                add_bias(r + 1, accs[r + 1])
+        add_bias(2, accs[2])
+        accs[4] = multiply(4)
+        accs[5] = multiply(5)
+        for i in range(R):
+            r = SEQ[i]
+            if i + 1 < R:
+                add_bias(SEQ[i + 1], accs[SEQ[i + 1]])
             row_max(r)
+            if i == 0:
+                quantise_h_pair(3)
+                nc.gpsimd.tensor_copy(
+                    out=h_codes[:, R : R + 2, 1:P], in_=h_codes[:, R - 2 : R, 0 : P - 1]
+                )
+                nc.gpsimd.tensor_copy(
+                    out=h_scales[:, R : R + 2, 1:P], in_=h_scales[:, R - 2 : R, 0 : P - 1]
+                )
+                for later in SEQ[4:]:
+                    accs[later] = multiply(later)
             ln_round()
             exp_and_sum(r)
             ln_round()

@@ -21,6 +21,7 @@ C = 512
 TAPS = 3
 R = ROWS // P
 FLOPS = 2 * ROWS * K * C * TAPS
+N_WARM = 4
 
 V_COLS = 320
 
@@ -80,6 +81,15 @@ def tile_predictor_pb_kernel(tc, H, W2, b2, out):
         shift = keep.tile([P, R], F32, name="shift")
         ln_row = keep.tile([P, R, N_LN_COLS], F32, name="ln_row")
 
+        warm = keep.tile([P, C], BF16, name="warm")
+        nc.vector.memset(warm[:], 0.0)
+        warm_ps = psum.tile([P, C], F32, name="warm_ps", tag="bank")
+
+        def keep_warm():
+            nc.tensor.matmul(warm_ps[:], lhsT=warm[:, 0:P], rhs=warm[:], start=True, stop=True)
+
+        for i in range(N_WARM):
+            keep_warm()
         make_identity(nc, ident[:])
         nc.vector.memset(b_row[:], 0.0)
         nc.vector.memset(threes[:], 3.0)
@@ -278,12 +288,14 @@ def tile_predictor_pb_kernel(tc, H, W2, b2, out):
 
         regroup_w(0)
         transpose_pair(0)
+        keep_warm()
         quantise_w(0)
         regroup_w(1)
         quantise_h_pair(0)
         transpose_pair(1)
         bias_ps = psum.tile([P, C], F32, name="bias_ps", tag="bank")
         nc.tensor.matmul(bias_ps[:], lhsT=threes[:], rhs=b_row[:], start=True, stop=True)
+        keep_warm()
         quantise_w(1)
         accs = {}
         accs[2] = new_acc()
@@ -296,6 +308,7 @@ def tile_predictor_pb_kernel(tc, H, W2, b2, out):
         nc.scalar.copy(out=bias[:], in_=bias_ps[:])
         quantise_w(2)
         transpose_pair(2)
+        keep_warm()
         transpose_pair(3)
         tap_pass(3, 1, accs[3])
         tap_pass(2, 2, accs[2])

@@ -118,7 +118,10 @@ def tile_predictor_pb_kernel(tc, H, W2, b2, out):
             nc.sync.dma_start(out=h_sb[:, pair, :], in_=h_view[:, pair, :])
 
         def load_w(j):
-            nc.sync.dma_start(out=w_raw[:, j], in_=W2[j].rearrange("(p t) c -> p t c", t=PACK))
+            nc.sync.dma_start(
+                out=w_raw[:, j].rearrange("p (u e) c -> p u e c", u=2),
+                in_=W2[j].rearrange("(u p e) c -> p u e c", u=2, e=2),
+            )
 
         load_w(0)
         load_h_pair(0)
@@ -129,7 +132,7 @@ def tile_predictor_pb_kernel(tc, H, W2, b2, out):
         load_h_pair(2)
         load_h_pair(3)
 
-        h_words = h_sb[:].bitcast(F32).rearrange("m r (p u) -> m r u p", u=2)
+        h_words = h_sb[:].bitcast(F32).rearrange("m r (u p) -> m r u p", u=2)
         h_grp_words = h_grp[:].bitcast(F32)
 
         def transpose_pair(a):

@@ -311,11 +311,10 @@ def tile_predictor_pb_kernel(tc, H, W2, b2, out):
         nc.scalar.copy(out=bias[:], in_=bias_ps[:])
         quantise_w(2)
         transpose_pair(2)
-        keep_warm()
-        transpose_pair(3)
         tap_pass(3, 1, accs[3])
         tap_pass(2, 2, accs[2])
         tap_pass(3, 2, accs[3])
+        transpose_pair(3)
         quantise_h_pair(2)
         add_bias(2, accs[2])
         accs[4] = multiply(4)

@@ -34,13 +34,15 @@ LN_BETA = 0.6138098239898682
 LN_ALPHA = 1.9999163150787354
 LN_LEVELS = 3
 SEQ = (2, 3, 4, 5, 6, 7, 0, 1)
+ELSEWHERE = SEQ[3]
 ON_VECTOR = SEQ[5:]
 
 K_GUESS = 0
-K_C1 = 1
+K_MINUS_C1 = 1
 K_MINUS_ALPHA = 2
 K_BETA = 3
-N_CONSTS = 4
+K_ONE = 4
+N_CONSTS = 5
 L_E0 = 0
 L_Q = 1
 L_T = 2
@@ -96,7 +98,8 @@ def tile_predictor_pb_kernel(tc, H, W2, b2, out):
         nc.vector.memset(h_codes[:, R : R + 2, :].bitcast(I32), 0)
         nc.vector.memset(h_scales[:].bitcast(I32), 0)
         nc.vector.memset(consts[:, K_GUESS : K_GUESS + 1], -LN_STEP * N_THR / 2.0)
-        nc.vector.memset(consts[:, K_C1 : K_C1 + 1], LN_C1)
+        nc.vector.memset(consts[:, K_MINUS_C1 : K_MINUS_C1 + 1], -LN_C1)
+        nc.vector.memset(consts[:, K_ONE : K_ONE + 1], 1.0)
         nc.vector.memset(consts[:, K_MINUS_ALPHA : K_MINUS_ALPHA + 1], -LN_ALPHA)
         nc.vector.memset(consts[:, K_BETA : K_BETA + 1], LN_BETA)
         nc.gpsimd.memset(thresholds[:, 0:1], EULER ** (LN_STEP / 2.0))
@@ -202,14 +205,6 @@ def tile_predictor_pb_kernel(tc, H, W2, b2, out):
             nc.vector.tensor_reduce(
                 out=neg_max[:, one], in_=z[:, r, :], axis=AX.X, op=ALU.max, negate=True
             )
-            nc.gpsimd.tensor_scalar(
-                out=neg_max_c[:, one],
-                in0=neg_max[:, one],
-                scalar1=-1.0,
-                scalar2=LN_STEP * N_THR / 2.0 + LN_C0,
-                op0=ALU.mult,
-                op1=ALU.add,
-            )
 
         def exp_and_sum(r):
             one = slice(r, r + 1)
@@ -220,6 +215,13 @@ def tile_predictor_pb_kernel(tc, H, W2, b2, out):
                 bias=neg_max[:, one],
                 scale=1.0,
                 accum_out=row_sum[:, one],
+            )
+            nc.scalar.activation(
+                out=neg_max_c[:, one],
+                in_=consts[:, K_ONE : K_ONE + 1],
+                func=ACT.Identity,
+                bias=neg_max[:, one],
+                scale=-(LN_STEP * N_THR / 2.0 + LN_C0),
             )
 
         def ln_level(r, level):
@@ -246,13 +248,13 @@ def tile_predictor_pb_kernel(tc, H, W2, b2, out):
                 )
                 nc.scalar.activation(
                     out=ln_row[:, r, L_C1_S : L_ALPHA_S + 1],
-                    in_=consts[:, K_C1 : K_MINUS_ALPHA + 1],
+                    in_=consts[:, K_MINUS_C1 : K_MINUS_ALPHA + 1],
                     func=ACT.Identity,
                     scale=s,
                 )
             elif level == 1:
                 act(ACT.Exp, col(L_E0), count[:, one], -LN_STEP / 2.0, const(K_GUESS))
-                act(ACT.Identity, col(L_Q), count[:, one], LN_STEP / 2.0, neg_max_c[:, one])
+                act(ACT.Identity, col(L_Q), count[:, one], -LN_STEP / 2.0, neg_max_c[:, one])
             elif level == 2:
                 act(ACT.Identity, col(L_T), col(L_E0), col(L_C1_S), col(L_Q))
                 act(ACT.Exp, col(L_B), col(L_E0), col(L_ALPHA_S), const(K_BETA))
@@ -262,12 +264,12 @@ def tile_predictor_pb_kernel(tc, H, W2, b2, out):
                         in0=z[:, r, :],
                         scalar1=col(L_T),
                         scalar2=col(L_B),
-                        op0=ALU.subtract,
+                        op0=ALU.add,
                         op1=ALU.add,
                     )
                     nc.sync.dma_start(out=out_view[:, r, :], in_=z[:, r, :])
             elif level == 3:
-                act(ACT.Identity, shift[:, one], col(L_T), -1.0, col(L_B))
+                act(ACT.Identity, shift[:, one], col(L_T), 1.0, col(L_B))
             else:
                 nc.gpsimd.tensor_scalar(
                     out=z[:, r, :],
@@ -321,7 +323,7 @@ def tile_predictor_pb_kernel(tc, H, W2, b2, out):
         accs[5] = multiply(5)
         for i in range(R):
             r = SEQ[i]
-            if i + 1 < R:
+            if i + 1 < R and SEQ[i + 1] != ELSEWHERE:
                 add_bias(SEQ[i + 1], accs[SEQ[i + 1]])
             row_max(r)
             if i == 0:
@@ -336,6 +338,11 @@ def tile_predictor_pb_kernel(tc, H, W2, b2, out):
                     accs[later] = multiply(later)
             ln_round()
             exp_and_sum(r)
+            if i == 0:
+                nc.scalar.copy(out=z[:, ELSEWHERE, :], in_=accs[ELSEWHERE][:])
+                nc.gpsimd.tensor_tensor(
+                    out=z[:, ELSEWHERE, :], in0=z[:, ELSEWHERE, :], in1=bias[:], op=ALU.add
+                )
             ln_round()
             summed.append(r)
         for level in range(LN_LEVELS):

@@ -26,30 +26,19 @@ N_WARM = 4
 V_COLS = 320
 
 EULER = 2.718281828459045
-N_THR = 128
-LN_STEP = 1591.0 / 32768.0
-LN_C0 = -0.2498800083345607
-LN_C1 = 0.49992698431015015
-LN_BETA = 0.6138098239898682
-LN_ALPHA = 1.9999163150787354
-LN_LEVELS = 3
+EULER_GAMMA = 0.5772156649015329
+N_DECAY = 64
+LOG_STEP = -0.75
+STEP = EULER ** LOG_STEP
+LN_SHIFT = -26.0
+T_0 = EULER ** (LN_SHIFT - EULER_GAMMA + STEP / 2.0)
 SEQ = (2, 3, 4, 5, 6, 7, 0, 1)
 ELSEWHERE = SEQ[3]
 ON_VECTOR = SEQ[5:]
 
-K_GUESS = 0
-K_MINUS_C1 = 1
-K_MINUS_ALPHA = 2
-K_BETA = 3
-K_ONE = 4
-N_CONSTS = 5
-L_E0 = 0
-L_Q = 1
-L_T = 2
-L_B = 3
-L_C1_S = 4
-L_ALPHA_S = 5
-N_LN_COLS = 6
+K_ONE = 0
+K_LOG_STEP = 1
+N_CONSTS = 2
 
 
 def tile_predictor_pb_kernel(tc, H, W2, b2, out):
@@ -73,15 +62,14 @@ def tile_predictor_pb_kernel(tc, H, W2, b2, out):
         w_scales = keep.tile([P, TAPS, C], U8, name="w_scales", align_bytes=64)
         z = keep.tile([P, R, C], F32, name="z")
         exp_out = keep.tile([P, C], BF16, name="exp_out")
-        sign_out = keep.tile([P, N_THR], BF16, name="sign_out")
+        decay_out = keep.tile([P, N_DECAY], BF16, name="decay_out")
         neg_max = keep.tile([P, R], F32, name="neg_max")
         neg_max_c = keep.tile([P, R], F32, name="neg_max_c")
-        thresholds = keep.tile([P, N_THR], F32, name="thresholds")
+        decay = keep.tile([P, N_DECAY], F32, name="decay")
         consts = keep.tile([P, N_CONSTS], F32, name="consts")
         row_sum = keep.tile([P, R], F32, name="row_sum")
-        count = keep.tile([P, R], F32, name="count")
+        decayed = keep.tile([P, R], F32, name="decayed")
         shift = keep.tile([P, R], F32, name="shift")
-        ln_row = keep.tile([P, R, N_LN_COLS], F32, name="ln_row")
 
         warm = keep.tile([P, C], BF16, name="warm")
         nc.vector.memset(warm[:], 0.0)
@@ -97,21 +85,18 @@ def tile_predictor_pb_kernel(tc, H, W2, b2, out):
         nc.vector.memset(threes[:], 3.0)
         nc.vector.memset(h_codes[:, R : R + 2, :].bitcast(I32), 0)
         nc.vector.memset(h_scales[:].bitcast(I32), 0)
-        nc.vector.memset(consts[:, K_GUESS : K_GUESS + 1], -LN_STEP * N_THR / 2.0)
-        nc.vector.memset(consts[:, K_MINUS_C1 : K_MINUS_C1 + 1], -LN_C1)
         nc.vector.memset(consts[:, K_ONE : K_ONE + 1], 1.0)
-        nc.vector.memset(consts[:, K_MINUS_ALPHA : K_MINUS_ALPHA + 1], -LN_ALPHA)
-        nc.vector.memset(consts[:, K_BETA : K_BETA + 1], LN_BETA)
-        nc.gpsimd.memset(thresholds[:, 0:1], EULER ** (LN_STEP / 2.0))
-        for width in (1, 2, 4, 8, 16, 32, 64):
+        nc.vector.memset(consts[:, K_LOG_STEP : K_LOG_STEP + 1], LOG_STEP)
+        nc.gpsimd.memset(decay[:, 1:2], 1.0)
+
+        def scaled_copy(dst, src, factor):
             nc.gpsimd.tensor_scalar(
-                out=thresholds[:, width : 2 * width],
-                in0=thresholds[:, 0:width],
-                scalar1=EULER ** (LN_STEP * width),
-                scalar2=0.0,
-                op0=ALU.mult,
-                op1=ALU.add,
+                out=decay[:, dst], in0=decay[:, src], scalar1=factor, scalar2=0.0, op0=ALU.mult, op1=ALU.add
             )
+
+        scaled_copy(slice(0, 1), slice(1, 2), -T_0)
+        for width in (1, 2, 4, 8, 16, 32):
+            scaled_copy(slice(width, 2 * width), slice(0, width), EULER ** (STEP * width))
 
         h_view = H.rearrange("(m r) k -> m r k", r=R)
         out_view = out.rearrange("(m r) c -> m r c", r=R)
@@ -221,75 +206,50 @@ def tile_predictor_pb_kernel(tc, H, W2, b2, out):
                 in_=consts[:, K_ONE : K_ONE + 1],
                 func=ACT.Identity,
                 bias=neg_max[:, one],
-                scale=-(LN_STEP * N_THR / 2.0 + LN_C0),
+                scale=LN_SHIFT,
             )
 
-        def ln_level(r, level):
+        def log_of_sum(r):
             one = slice(r, r + 1)
-            s = row_sum[:, one]
+            nc.scalar.activation(
+                out=decay_out[:],
+                in_=decay[:],
+                func=ACT.Exp,
+                bias=consts[:, K_LOG_STEP : K_LOG_STEP + 1],
+                scale=row_sum[:, one],
+                accum_out=decayed[:, one],
+            )
 
-            def col(i):
-                return ln_row[:, r, i : i + 1]
+        def finish_on_vector(r):
+            one = slice(r, r + 1)
+            nc.vector.tensor_scalar(
+                out=z[:, r, :],
+                in0=z[:, r, :],
+                scalar1=neg_max_c[:, one],
+                scalar2=decayed[:, one],
+                op0=ALU.add,
+                op1=ALU.add,
+            )
+            nc.sync.dma_start(out=out_view[:, r, :], in_=z[:, r, :])
 
-            def const(i):
-                return consts[:, i : i + 1]
-
-            def act(func, dst, src, scale, offset):
-                nc.scalar.activation(out=dst, in_=src, func=func, bias=offset, scale=scale)
-
-            if level == 0:
-                nc.scalar.activation(
-                    out=sign_out[:],
-                    in_=thresholds[:],
-                    func=ACT.Sign,
-                    bias=s,
-                    scale=-1.0,
-                    accum_out=count[:, one],
-                )
-                nc.scalar.activation(
-                    out=ln_row[:, r, L_C1_S : L_ALPHA_S + 1],
-                    in_=consts[:, K_MINUS_C1 : K_MINUS_ALPHA + 1],
-                    func=ACT.Identity,
-                    scale=s,
-                )
-            elif level == 1:
-                act(ACT.Exp, col(L_E0), count[:, one], -LN_STEP / 2.0, const(K_GUESS))
-                act(ACT.Identity, col(L_Q), count[:, one], -LN_STEP / 2.0, neg_max_c[:, one])
-            elif level == 2:
-                act(ACT.Identity, col(L_T), col(L_E0), col(L_C1_S), col(L_Q))
-                act(ACT.Exp, col(L_B), col(L_E0), col(L_ALPHA_S), const(K_BETA))
-                if r in ON_VECTOR:
-                    nc.vector.tensor_scalar(
-                        out=z[:, r, :],
-                        in0=z[:, r, :],
-                        scalar1=col(L_T),
-                        scalar2=col(L_B),
-                        op0=ALU.add,
-                        op1=ALU.add,
-                    )
-                    nc.sync.dma_start(out=out_view[:, r, :], in_=z[:, r, :])
-            elif level == 3:
-                act(ACT.Identity, shift[:, one], col(L_T), 1.0, col(L_B))
-            else:
-                nc.gpsimd.tensor_scalar(
-                    out=z[:, r, :],
-                    in0=z[:, r, :],
-                    scalar1=shift[:, one],
-                    scalar2=1.0,
-                    op0=ALU.add,
-                    op1=ALU.mult,
-                )
-                nc.sync.dma_start(out=out_view[:, r, :], in_=z[:, r, :])
-
-        levels = [LN_LEVELS if r in ON_VECTOR else LN_LEVELS + 2 for r in range(R)]
-        next_level = [0] * R
-        summed = []
-
-        def ln_round():
-            for r in reversed(summed):
-                if next_level[r] < levels[r]:
-                    ln_level(r, next_level[r])
-                    next_level[r] = next_level[r] + 1
+        def finish_on_gpsimd(r):
+            one = slice(r, r + 1)
+            nc.scalar.activation(
+                out=shift[:, one],
+                in_=decayed[:, one],
+                func=ACT.Identity,
+                bias=neg_max_c[:, one],
+                scale=1.0,
+            )
+            nc.gpsimd.tensor_scalar(
+                out=z[:, r, :],
+                in0=z[:, r, :],
+                scalar1=shift[:, one],
+                scalar2=1.0,
+                op0=ALU.add,
+                op1=ALU.mult,
+            )
+            nc.sync.dma_start(out=out_view[:, r, :], in_=z[:, r, :])
 
         regroup_w(0)
         transpose_pair(0)
@@ -336,14 +296,14 @@ def tile_predictor_pb_kernel(tc, H, W2, b2, out):
                 )
                 for later in SEQ[4:]:
                     accs[later] = multiply(later)
-            ln_round()
             exp_and_sum(r)
             if i == 0:
                 nc.scalar.copy(out=z[:, ELSEWHERE, :], in_=accs[ELSEWHERE][:])
                 nc.gpsimd.tensor_tensor(
                     out=z[:, ELSEWHERE, :], in0=z[:, ELSEWHERE, :], in1=bias[:], op=ALU.add
                 )
-            ln_round()
-            summed.append(r)
-        for level in range(LN_LEVELS):
-            ln_round()
+            elif SEQ[i - 1] not in ON_VECTOR:
+                finish_on_gpsimd(SEQ[i - 1])
+            log_of_sum(r)
+        for r in ON_VECTOR:
+            finish_on_vector(r)

@@ -33,7 +33,7 @@ STEP = EULER ** LOG_STEP
 LN_SHIFT = -26.0
 T_0 = EULER ** (LN_SHIFT - EULER_GAMMA + STEP / 2.0)
 SEQ = (2, 3, 4, 5, 6, 7, 0, 1)
-ELSEWHERE = SEQ[3]
+LAST = SEQ[R - 1]
 ON_VECTOR = SEQ[5:]
 
 K_ONE = 0
@@ -113,9 +113,9 @@ def tile_predictor_pb_kernel(tc, H, W2, b2, out):
 
         load_w(0)
         load_h_pair(0)
+        load_w(1)
         load_h_pair(1)
         nc.sync.dma_start(out=b_row[0:1, :], in_=b2)
-        load_w(1)
         load_w(2)
         load_h_pair(2)
         load_h_pair(3)
@@ -201,6 +201,9 @@ def tile_predictor_pb_kernel(tc, H, W2, b2, out):
                 scale=1.0,
                 accum_out=row_sum[:, one],
             )
+
+        def shifted_max(r):
+            one = slice(r, r + 1)
             nc.scalar.activation(
                 out=neg_max_c[:, one],
                 in_=consts[:, K_ONE : K_ONE + 1],
@@ -234,12 +237,8 @@ def tile_predictor_pb_kernel(tc, H, W2, b2, out):
 
         def finish_on_gpsimd(r):
             one = slice(r, r + 1)
-            nc.scalar.activation(
-                out=shift[:, one],
-                in_=decayed[:, one],
-                func=ACT.Identity,
-                bias=neg_max_c[:, one],
-                scale=1.0,
+            nc.gpsimd.tensor_tensor(
+                out=shift[:, one], in0=decayed[:, one], in1=neg_max_c[:, one], op=ALU.add
             )
             nc.gpsimd.tensor_scalar(
                 out=z[:, r, :],
@@ -283,8 +282,10 @@ def tile_predictor_pb_kernel(tc, H, W2, b2, out):
         accs[5] = multiply(5)
         for i in range(R):
             r = SEQ[i]
-            if i + 1 < R and SEQ[i + 1] != ELSEWHERE:
+            if i + 1 < R and SEQ[i + 1] != LAST:
                 add_bias(SEQ[i + 1], accs[SEQ[i + 1]])
+            if r == LAST:
+                add_bias(r, accs[r])
             row_max(r)
             if i == 0:
                 quantise_h_pair(3)
@@ -297,13 +298,16 @@ def tile_predictor_pb_kernel(tc, H, W2, b2, out):
                 for later in SEQ[4:]:
                     accs[later] = multiply(later)
             exp_and_sum(r)
-            if i == 0:
-                nc.scalar.copy(out=z[:, ELSEWHERE, :], in_=accs[ELSEWHERE][:])
-                nc.gpsimd.tensor_tensor(
-                    out=z[:, ELSEWHERE, :], in0=z[:, ELSEWHERE, :], in1=bias[:], op=ALU.add
-                )
-            elif SEQ[i - 1] not in ON_VECTOR:
-                finish_on_gpsimd(SEQ[i - 1])
-            log_of_sum(r)
+            if r not in ON_VECTOR:
+                shifted_max(r)
+                log_of_sum(r)
+                finish_on_gpsimd(r)
+            elif r == SEQ[R - 2]:
+                for earlier in ON_VECTOR[:-1]:
+                    shifted_max(earlier)
+                for earlier in ON_VECTOR[:-1]:
+                    log_of_sum(earlier)
+        shifted_max(LAST)
+        log_of_sum(LAST)
         for r in ON_VECTOR:
             finish_on_vector(r)

@@ -253,12 +253,14 @@ def tile_predictor_pb_kernel(tc, H, W2, b2, out):
         regroup_w(0)
         transpose_pair(0)
         keep_warm()
+        keep_warm()
         quantise_w(0)
         regroup_w(1)
         quantise_h_pair(0)
         transpose_pair(1)
         bias_ps = psum.tile([P, C], F32, name="bias_ps", tag="bank")
         nc.tensor.matmul(bias_ps[:], lhsT=threes[:], rhs=b_row[:], start=True, stop=True)
+        keep_warm()
         keep_warm()
         quantise_w(1)
         accs = {}

@@ -34,7 +34,7 @@ LN_SHIFT = -26.0
 T_0 = EULER ** (LN_SHIFT - EULER_GAMMA + STEP / 2.0)
 SEQ = (2, 3, 4, 5, 6, 7, 0, 1)
 LAST = SEQ[R - 1]
-ON_VECTOR = SEQ[5:]
+ON_VECTOR = SEQ[4:]
 
 K_ONE = 0
 K_LOG_STEP = 1
@@ -288,6 +288,7 @@ def tile_predictor_pb_kernel(tc, H, W2, b2, out):
                 add_bias(SEQ[i + 1], accs[SEQ[i + 1]])
             if r == LAST:
                 add_bias(r, accs[r])
+                finish_on_vector(ON_VECTOR[0])
             row_max(r)
             if i == 0:
                 quantise_h_pair(3)
@@ -300,16 +301,17 @@ def tile_predictor_pb_kernel(tc, H, W2, b2, out):
                 for later in SEQ[4:]:
                     accs[later] = multiply(later)
             exp_and_sum(r)
-            if r not in ON_VECTOR:
+            if r not in SEQ[5:]:
                 shifted_max(r)
                 log_of_sum(r)
-                finish_on_gpsimd(r)
+                if r not in ON_VECTOR:
+                    finish_on_gpsimd(r)
             elif r == SEQ[R - 2]:
-                for earlier in ON_VECTOR[:-1]:
+                for earlier in SEQ[5:7]:
                     shifted_max(earlier)
-                for earlier in ON_VECTOR[:-1]:
+                for earlier in SEQ[5:7]:
                     log_of_sum(earlier)
         shifted_max(LAST)
         log_of_sum(LAST)
-        for r in ON_VECTOR:
+        for r in ON_VECTOR[1:]:
             finish_on_vector(r)

@@ -32,7 +32,8 @@ LOG_STEP = -0.75
 STEP = EULER ** LOG_STEP
 LN_SHIFT = -26.0
 T_0 = EULER ** (LN_SHIFT - EULER_GAMMA + STEP / 2.0)
-SEQ = (2, 3, 4, 5, 6, 7, 0, 1)
+SEQ = (2, 3, 5, 4, 6, 7, 0, 1)
+ELSEWHERE = SEQ[3]
 LAST = SEQ[R - 1]
 ON_VECTOR = SEQ[4:]
 
@@ -274,30 +275,30 @@ def tile_predictor_pb_kernel(tc, H, W2, b2, out):
         nc.scalar.copy(out=bias[:], in_=bias_ps[:])
         quantise_w(2)
         transpose_pair(2)
+        transpose_pair(3)
         tap_pass(3, 1, accs[3])
         tap_pass(2, 2, accs[2])
         tap_pass(3, 2, accs[3])
-        transpose_pair(3)
         quantise_h_pair(2)
         add_bias(2, accs[2])
+        quantise_h_pair(3)
+        nc.gpsimd.tensor_copy(out=h_codes[:, R : R + 2, 1:P], in_=h_codes[:, R - 2 : R, 0 : P - 1])
+        nc.gpsimd.tensor_copy(out=h_scales[:, R : R + 2, 1:P], in_=h_scales[:, R - 2 : R, 0 : P - 1])
         accs[4] = multiply(4)
         accs[5] = multiply(5)
+        nc.scalar.copy(out=z[:, ELSEWHERE, :], in_=accs[ELSEWHERE][:])
+        nc.gpsimd.tensor_tensor(
+            out=z[:, ELSEWHERE, :], in0=z[:, ELSEWHERE, :], in1=bias[:], op=ALU.add
+        )
         for i in range(R):
             r = SEQ[i]
-            if i + 1 < R and SEQ[i + 1] != LAST:
+            if i + 1 < R and SEQ[i + 1] not in (ELSEWHERE, LAST):
                 add_bias(SEQ[i + 1], accs[SEQ[i + 1]])
             if r == LAST:
                 add_bias(r, accs[r])
                 finish_on_vector(ON_VECTOR[0])
             row_max(r)
             if i == 0:
-                quantise_h_pair(3)
-                nc.gpsimd.tensor_copy(
-                    out=h_codes[:, R : R + 2, 1:P], in_=h_codes[:, R - 2 : R, 0 : P - 1]
-                )
-                nc.gpsimd.tensor_copy(
-                    out=h_scales[:, R : R + 2, 1:P], in_=h_scales[:, R - 2 : R, 0 : P - 1]
-                )
                 for later in SEQ[4:]:
                     accs[later] = multiply(later)
             exp_and_sum(r)

@@ -153,11 +153,12 @@ def tile_predictor_pb_kernel(tc, H, W2, b2, out):
                 )
 
         def quantise_w(j):
-            nc.vector.quantize_mx(
-                out=w_codes[:, j, :].bitcast(FP8X4),
-                scales=w_scales[:, j, :],
-                in_=w_grp[:, j].rearrange("p c t -> p (c t)"),
-            )
+            for c0 in (0, C // 2):
+                nc.vector.quantize_mx(
+                    out=w_codes[:, j, c0 : c0 + C // 2].bitcast(FP8X4),
+                    scales=w_scales[:, j, c0 : c0 + C // 2],
+                    in_=w_grp[:, j, c0 : c0 + C // 2].rearrange("p c t -> p (c t)"),
+                )
 
         def new_acc():
             acc = psum.tile([P, C], F32, name="acc", tag="bank")
@@ -272,8 +273,8 @@ def tile_predictor_pb_kernel(tc, H, W2, b2, out):
         tap_pass(2, 1, accs[2])
         regroup_w(2)
         quantise_h_pair(1)
-        nc.scalar.copy(out=bias[:], in_=bias_ps[:])
         quantise_w(2)
+        nc.vector.tensor_copy(out=bias[:], in_=bias_ps[:])
         transpose_pair(2)
         transpose_pair(3)
         tap_pass(3, 1, accs[3])

from contextlib import ExitStack

import concourse.mybir as mybir
from concourse.masks import make_identity

F32 = mybir.dt.float32
BF16 = mybir.dt.bfloat16
U32 = mybir.dt.uint32
U8 = mybir.dt.uint8
I32 = mybir.dt.int32
FP8X4 = mybir.dt.float8_e4m3fn_x4
ALU = mybir.AluOpType
ACT = mybir.ActivationFunctionType
AX = mybir.AxisListType

P = 128
PACK = 4
ROWS = 1024
K = 512
C = 512
TAPS = 3
R = ROWS // P
FLOPS = 2 * ROWS * K * C * TAPS
N_WARM = 4

V_COLS = 320

EULER = 2.718281828459045
EULER_GAMMA = 0.5772156649015329
N_DECAY = 64
LOG_STEP = -0.75
STEP = EULER ** LOG_STEP
LN_SHIFT = -26.0
T_0 = EULER ** (LN_SHIFT - EULER_GAMMA + STEP / 2.0)
SEQ = (2, 3, 5, 4, 6, 7, 0, 1)
ELSEWHERE = SEQ[3]
LAST = SEQ[R - 1]
ON_VECTOR = SEQ[4:]

K_ONE = 0
K_LOG_STEP = 1
N_CONSTS = 2


def tile_predictor_pb_kernel(tc, H, W2, b2, out):
    nc = tc.nc
    with ExitStack() as ctx:
        keep = ctx.enter_context(tc.tile_pool(name="keep", bufs=1))
        psum = ctx.enter_context(tc.psum_pool(name="psum", bufs=8))
        ctx.enter_context(tc.manual_schedule())

        ident = keep.tile([P, P], F32, name="ident")
        h_sb = keep.tile([P, R, K], BF16, name="h_sb")
        w_raw = keep.tile([P, TAPS, PACK, C], BF16, name="w_raw")
        b_row = keep.tile([P, C], BF16, name="b_row")
        threes = keep.tile([P, P], BF16, name="threes")
        bias = keep.tile([P, C], F32, name="bias")
        h_grp = keep.tile([P, R, P, PACK], BF16, name="h_grp", align_bytes=64)
        w_grp = keep.tile([P, TAPS, C, PACK], BF16, name="w_grp", align_bytes=64)
        h_codes = keep.tile([P, R + 2, P], U32, name="h_codes", align_bytes=64)
        h_scales = keep.tile([P, R + 2, P], U8, name="h_scales", align_bytes=64)
        w_codes = keep.tile([P, TAPS, C], U32, name="w_codes", align_bytes=64)
        w_scales = keep.tile([P, TAPS, C], U8, name="w_scales", align_bytes=64)
        z = keep.tile([P, R, C], F32, name="z")
        exp_out = keep.tile([P, C], BF16, name="exp_out")
        decay_out = keep.tile([P, N_DECAY], BF16, name="decay_out")
        neg_max = keep.tile([P, R], F32, name="neg_max")
        neg_max_c = keep.tile([P, R], F32, name="neg_max_c")
        decay = keep.tile([P, N_DECAY], F32, name="decay")
        consts = keep.tile([P, N_CONSTS], F32, name="consts")
        row_sum = keep.tile([P, R], F32, name="row_sum")
        decayed = keep.tile([P, R], F32, name="decayed")
        shift = keep.tile([P, R], F32, name="shift")

        warm = keep.tile([P, C], BF16, name="warm")
        nc.vector.memset(warm[:], 0.0)
        warm_ps = psum.tile([P, C], F32, name="warm_ps", tag="bank")

        def keep_warm():
            nc.tensor.matmul(warm_ps[:], lhsT=warm[:, 0:P], rhs=warm[:], start=True, stop=True)

        for i in range(N_WARM):
            keep_warm()
        make_identity(nc, ident[:])
        nc.vector.memset(b_row[:], 0.0)
        nc.vector.memset(threes[:], 3.0)
        nc.vector.memset(h_codes[:, R : R + 2, :].bitcast(I32), 0)
        nc.vector.memset(h_scales[:].bitcast(I32), 0)
        nc.vector.memset(consts[:, K_ONE : K_ONE + 1], 1.0)
        nc.vector.memset(consts[:, K_LOG_STEP : K_LOG_STEP + 1], LOG_STEP)
        nc.gpsimd.memset(decay[:, 1:2], 1.0)

        def scaled_copy(dst, src, factor):
            nc.gpsimd.tensor_scalar(
                out=decay[:, dst], in0=decay[:, src], scalar1=factor, scalar2=0.0, op0=ALU.mult, op1=ALU.add
            )

        scaled_copy(slice(0, 1), slice(1, 2), -T_0)
        for width in (1, 2, 4, 8, 16, 32):
            scaled_copy(slice(width, 2 * width), slice(0, width), EULER ** (STEP * width))

        h_view = H.rearrange("(m r) k -> m r k", r=R)
        out_view = out.rearrange("(m r) c -> m r c", r=R)

        def load_h_pair(a):
            pair = slice(2 * a, 2 * a + 2)
            nc.sync.dma_start(out=h_sb[:, pair, :], in_=h_view[:, pair, :])

        def load_w(j):
            nc.sync.dma_start(
                out=w_raw[:, j].rearrange("p (u e) c -> p u e c", u=2),
                in_=W2[j].rearrange("(u p e) c -> p u e c", u=2, e=2),
            )

        load_w(0)
        load_h_pair(0)
        load_w(1)
        load_h_pair(1)
        nc.sync.dma_start(out=b_row[0:1, :], in_=b2)
        load_w(2)
        load_h_pair(2)
        load_h_pair(3)

        h_words = h_sb[:].bitcast(F32).rearrange("m r (u p) -> m r u p", u=2)
        h_grp_words = h_grp[:].bitcast(F32)

        def transpose_pair(a):
            flipped = psum.tile([P, 2, 2, P], F32, name="flipped", tag="bank")
            for i in range(2):
                for u in range(2):
                    nc.tensor.transpose(flipped[:, i, u, :], h_words[:, 2 * a + i, u, :], ident[:])
            nc.scalar.copy(
                out=h_grp_words[:, 2 * a : 2 * a + 2, :, :],
                in_=flipped[:].rearrange("p i u m -> p i m u"),
            )
            return flipped

        def quantise_h(grouped, first):
            nc.vector.quantize_mx(
                out=h_codes[:, first : first + 2, :].rearrange("p i m -> p (i m)").bitcast(FP8X4),
                scales=h_scales[:, first : first + 2, :].rearrange("p i m -> p (i m)"),
                in_=grouped.rearrange("p i m t -> p (i m t)"),
            )

        def quantise_h_pair(a):
            quantise_h(h_grp[:, 2 * a : 2 * a + 2], 2 * a)

        def regroup_w(j):
            for copy, c0, c1 in ((nc.vector.tensor_copy, 0, V_COLS), (nc.scalar.copy, V_COLS, C)):
                copy(
                    out=w_grp[:, j, c0:c1, :].rearrange("p (c i) t -> p c t i", i=4),
                    in_=w_raw[:, j, :, c0:c1].rearrange("p t (c i) -> p c t i", i=4),
                )

        def quantise_w(j):
            for c0 in (0, C // 2):
                nc.vector.quantize_mx(
                    out=w_codes[:, j, c0 : c0 + C // 2].bitcast(FP8X4),
                    scales=w_scales[:, j, c0 : c0 + C // 2],
                    in_=w_grp[:, j, c0 : c0 + C // 2].rearrange("p c t -> p (c t)"),
                )

        def new_acc():
            acc = psum.tile([P, C], F32, name="acc", tag="bank")
            return acc

        def tap_pass(r, j, acc):
            source = r - (TAPS - 1 - j)
            if source < 0:
                source = R + 2 + source
            nc.tensor.matmul_mx(
                out=acc[:],
                lhsT=h_codes[:, source, :].bitcast(FP8X4),
                lhsT_scale=h_scales[:, source, :],
                rhs=w_codes[:, j, :].bitcast(FP8X4),
                rhs_scale=w_scales[:, j, :],
                start=(j == 0),
                stop=(j == TAPS - 1),
            )

        def multiply(r):
            acc = new_acc()
            for j in range(TAPS):
                tap_pass(r, j, acc)
            return acc

        def add_bias(r, acc):
            nc.vector.tensor_tensor(out=z[:, r, :], in0=acc[:], in1=bias[:], op=ALU.add)

        def row_max(r):
            one = slice(r, r + 1)
            nc.vector.tensor_reduce(
                out=neg_max[:, one], in_=z[:, r, :], axis=AX.X, op=ALU.max, negate=True
            )

        def exp_and_sum(r):
            one = slice(r, r + 1)
            nc.scalar.activation(
                out=exp_out[:],
                in_=z[:, r, :],
                func=ACT.Exp,
                bias=neg_max[:, one],
                scale=1.0,
                accum_out=row_sum[:, one],
            )

        def shifted_max(r):
            one = slice(r, r + 1)
            nc.scalar.activation(
                out=neg_max_c[:, one],
                in_=consts[:, K_ONE : K_ONE + 1],
                func=ACT.Identity,
                bias=neg_max[:, one],
                scale=LN_SHIFT,
            )

        def log_of_sum(r):
            one = slice(r, r + 1)
            nc.scalar.activation(
                out=decay_out[:],
                in_=decay[:],
                func=ACT.Exp,
                bias=consts[:, K_LOG_STEP : K_LOG_STEP + 1],
                scale=row_sum[:, one],
                accum_out=decayed[:, one],
            )

        def finish_on_vector(r):
            one = slice(r, r + 1)
            nc.vector.tensor_scalar(
                out=z[:, r, :],
                in0=z[:, r, :],
                scalar1=neg_max_c[:, one],
                scalar2=decayed[:, one],
                op0=ALU.add,
                op1=ALU.add,
            )
            nc.sync.dma_start(out=out_view[:, r, :], in_=z[:, r, :])

        def finish_on_gpsimd(r):
            one = slice(r, r + 1)
            nc.gpsimd.tensor_tensor(
                out=shift[:, one], in0=decayed[:, one], in1=neg_max_c[:, one], op=ALU.add
            )
            nc.gpsimd.tensor_scalar(
                out=z[:, r, :],
                in0=z[:, r, :],
                scalar1=shift[:, one],
                scalar2=1.0,
                op0=ALU.add,
                op1=ALU.mult,
            )
            nc.sync.dma_start(out=out_view[:, r, :], in_=z[:, r, :])

        regroup_w(0)
        transpose_pair(0)
        keep_warm()
        keep_warm()
        quantise_w(0)
        regroup_w(1)
        quantise_h_pair(0)
        transpose_pair(1)
        bias_ps = psum.tile([P, C], F32, name="bias_ps", tag="bank")
        nc.tensor.matmul(bias_ps[:], lhsT=threes[:], rhs=b_row[:], start=True, stop=True)
        keep_warm()
        keep_warm()
        quantise_w(1)
        accs = {}
        accs[2] = new_acc()
        accs[3] = new_acc()
        tap_pass(2, 0, accs[2])
        tap_pass(3, 0, accs[3])
        tap_pass(2, 1, accs[2])
        regroup_w(2)
        quantise_h_pair(1)
        quantise_w(2)
        nc.vector.tensor_copy(out=bias[:], in_=bias_ps[:])
        transpose_pair(2)
        transpose_pair(3)
        tap_pass(3, 1, accs[3])
        tap_pass(2, 2, accs[2])
        tap_pass(3, 2, accs[3])
        quantise_h_pair(2)
        add_bias(2, accs[2])
        quantise_h_pair(3)
        nc.gpsimd.tensor_copy(out=h_codes[:, R : R + 2, 1:P], in_=h_codes[:, R - 2 : R, 0 : P - 1])
        nc.gpsimd.tensor_copy(out=h_scales[:, R : R + 2, 1:P], in_=h_scales[:, R - 2 : R, 0 : P - 1])
        accs[4] = multiply(4)
        accs[5] = multiply(5)
        nc.scalar.copy(out=z[:, ELSEWHERE, :], in_=accs[ELSEWHERE][:])
        nc.gpsimd.tensor_tensor(
            out=z[:, ELSEWHERE, :], in0=z[:, ELSEWHERE, :], in1=bias[:], op=ALU.add
        )
        for i in range(R):
            r = SEQ[i]
            if i + 1 < R and SEQ[i + 1] not in (ELSEWHERE, LAST):
                add_bias(SEQ[i + 1], accs[SEQ[i + 1]])
            if r == LAST:
                add_bias(r, accs[r])
                finish_on_vector(ON_VECTOR[0])
            row_max(r)
            if i == 0:
                for later in SEQ[4:]:
                    accs[later] = multiply(later)
            exp_and_sum(r)
            if r not in SEQ[5:]:
                shifted_max(r)
                log_of_sum(r)
                if r not in ON_VECTOR:
                    finish_on_gpsimd(r)
            elif r == SEQ[R - 2]:
                for earlier in SEQ[5:7]:
                    shifted_max(earlier)
                for earlier in SEQ[5:7]:
                    log_of_sum(earlier)
        shifted_max(LAST)
        log_of_sum(LAST)
        for r in ON_VECTOR[1:]:
            finish_on_vector(r)
